import numpy as np
import ml_dtypes


def mxq(x, axis, fmt="e4m3"):
    dtype, down = {"e4m3": (ml_dtypes.float8_e4m3fn, 7), "e5m2": (ml_dtypes.float8_e5m2, 14)}[fmt]
    v = np.moveaxis(np.asarray(x, np.float32).astype(ml_dtypes.bfloat16).astype(np.float64), axis, -1)
    blocks = v.reshape(v.shape[:-1] + (-1, 32))
    amax = np.abs(blocks).max(-1, keepdims=True)
    byte = np.maximum(np.where(amax > 0, np.frexp(amax)[1] - 1 + 127, 0) - down, 1)
    scale = np.exp2(byte - 127.0)
    codes = (blocks / scale).astype(np.float32).astype(dtype).astype(np.float64)
    return np.moveaxis((codes * scale).reshape(v.shape), -1, axis)


WIDE = False


def mx_kscale(k):
    if not WIDE:
        return np.ones(k)
    levels = np.array([10, -10, 5, -5, 0])
    if k % 512:
        return np.exp2(np.random.permutation(np.resize(levels, k // 32))).repeat(32)
    a = np.empty((k // 512, 16))
    for p in range(k // 512):
        a[p, :8] = np.random.permutation(np.resize(levels, 8))
        for g in range(8):
            far = levels[np.abs(levels - a[p, g]) >= 10]
            a[p, g + 8] = far[np.random.randint(len(far))]
    return np.exp2(a.ravel()).repeat(32)


BF16 = ml_dtypes.bfloat16


def bf(x):
    return np.asarray(x, np.float32).astype(BF16)


def f64(x):
    return np.asarray(x).astype(np.float64)


B, C, H, W = 2, 512, 64, 64
N = H * W
KV = 0.05 * N / np.sqrt(C)


def draw0():
    s, t = mx_kscale(C), mx_kscale(C)
    return {"x": bf(np.random.standard_normal((B, C, H, W)) * s[None, :, None, None]),
            "mask": bf(np.random.random_sample((B, 1, H, W))),
            "W_q": bf(np.random.standard_normal((C, C)) / np.sqrt(C) / s[:, None]),
            "b_q": bf(np.random.standard_normal(C) * 0.3),
            "kv_know": bf(np.random.standard_normal((B, 1, C)) * KV * t),
            "kv_mask": bf(np.random.standard_normal((B, 1, C)) * KV * t),
            "W_out": bf(np.random.standard_normal((C, C)) / KV / t[:, None]),
            "b_out": bf(np.random.standard_normal(C) * 0.2)}


def core(x, mask, W_q, b_q, kv_know, kv_mask, W_out, b_out):
    x, mask = f64(x), f64(mask)
    b, c, h, w = x.shape
    xf = np.transpose(x, (0, 2, 3, 1)).reshape(b, h * w, c)
    q = (mxq(xf, 2, "e4m3") @ mxq(f64(W_q), 0, "e4m3")) + f64(b_q)
    q = q / np.linalg.norm(q, axis=-1, keepdims=True)
    m = np.transpose(mask, (0, 2, 3, 1)).reshape(b, h * w, 1)
    inv = 1.0 - m
    qu = q * inv
    qm = q * m
    out_know = f64(kv_know) * qu
    out_mask = f64(kv_mask) * qm
    out = out_know * inv + m * (0.3 * out_know + 0.7 * out_mask)
    return (mxq(out, 2, "e4m3") @ mxq(f64(W_out), 0, "e4m3")) + f64(b_out)


def e4m3fn_bytes(y):
    return np.clip(np.asarray(y, np.float64), -448.0, 448.0).astype(np.float32).astype(ml_dtypes.float8_e4m3fn).view(np.uint8)


def e4m3fn_values(b):
    return np.asarray(b, np.uint8).view(ml_dtypes.float8_e4m3fn).astype(np.float64)


def setup_inputs():
    d = draw0()
    x0 = np.asarray(d['x']).astype(np.float64)
    s = (np.max(np.abs(x0), axis=(0, 2, 3), keepdims=True) / 448.0).astype(np.float32)
    out = {}
    for k, v in d.items():
        if k == 'x':
            out['x_bytes'] = e4m3fn_bytes(x0 / s.astype(np.float64))
            out['x_scale'] = s
        else:
            out[k] = v
    return out


def reference(x_bytes, x_scale, mask, W_q, b_q, kv_know, kv_mask, W_out, b_out):
    return core(e4m3fn_values(x_bytes) * x_scale.astype(np.float64), mask, W_q, b_q, kv_know, kv_mask, W_out, b_out)

@@ -1,0 +1,416 @@
+from contextlib import ExitStack
+
+import concourse.mybir as mybir
+from concourse.masks import make_identity
+
+F32 = mybir.dt.float32
+BF16 = mybir.dt.bfloat16
+U32 = mybir.dt.uint32
+U8 = mybir.dt.uint8
+FP8 = mybir.dt.float8_e4m3fn
+FP8X4 = mybir.dt.float8_e4m3fn_x4
+ALU = mybir.AluOpType
+ACT = mybir.ActivationFunctionType
+AXIS = mybir.AxisListType
+
+B = 2
+C = 512
+N = 4096
+P = 128
+PACK = 4
+TILE = 128
+CHUNK = 512
+NT = CHUNK // TILE
+NTILES = B * N // TILE
+NCHUNKS = B * N // CHUNK
+PER_IMG = N // CHUNK
+BLK = 16
+Q = 8
+
+FLOPS = 2 * 2 * B * N * C * C
+
+X_LOADS = ((0, 0, 512), (0, 512, 512), (0, 1024, 1024), (0, 2048, 2048), (1, 0, 2048), (1, 2048, 2048))
+FIRST_SBUF_GATE = 3
+
+
+def tile_hydraattention_pb_t_kernel(tc, x_bytes, x_scale, mask, W_q, b_q, kv_know, kv_mask, W_out, b_out, out):
+    nc = tc.nc
+    out_rows = out.rearrange("b t c -> (b t) c")
+
+    with ExitStack() as ctx:
+        keep = ctx.enter_context(tc.tile_pool(name="keep", bufs=1))
+        work = ctx.enter_context(tc.tile_pool(name="work", bufs=3))
+        psum = ctx.enter_context(tc.psum_pool(name="psum", bufs=2))
+        ctx.enter_context(tc.manual_schedule())
+
+        xs = keep.tile([P, PACK], F32, name="xs")
+        nc.sync.dma_start(out=xs[:], in_=x_scale.rearrange("o (p j) a b -> p (o j a b)", j=PACK))
+        x_tiles = []
+
+        def load_x(i):
+            img, t0, width = X_LOADS[i]
+            t = keep.tile([P, PACK, width], U8, name=f"xb{i}", align_bytes=64)
+            nc.sync.dma_start(out=t[:], in_=x_bytes[img].rearrange("(p j) h w -> p j (h w)", j=PACK)[:, :, t0 : t0 + width])
+            x_tiles.append((img * N + t0, width, t))
+
+        load_x(0)
+        wq_raw = keep.tile([P, PACK, C], BF16, name="wq_raw")
+        nc.sync.dma_start(out=wq_raw[:], in_=W_q.rearrange("(p j) w -> p j w", j=PACK))
+        mrow = keep.tile([P, P], BF16, name="mrow")
+        nc.vector.memset(mrow[:], 0.0)
+        nc.sync.dma_start(out=mrow[0:NTILES, :], in_=mask.rearrange("b o (r q) w -> (b o r) (q w)", q=2))
+        bq_raw = keep.tile([P, C], BF16, name="bq_raw")
+        nc.sync.dma_start(out=bq_raw[:], in_=b_q.partition_broadcast(P))
+        kv_raw = []
+
+        def load_kv(img):
+            a = keep.tile([P, C], BF16, name=f"kvk_raw{img}")
+            nc.sync.dma_start(out=a[:], in_=kv_know[img].rearrange("o c -> (o c)").partition_broadcast(P))
+            b = keep.tile([P, C], BF16, name=f"kvm_raw{img}")
+            nc.sync.dma_start(out=b[:], in_=kv_mask[img].rearrange("o c -> (o c)").partition_broadcast(P))
+            kv_raw.append((a, b))
+
+        load_kv(0)
+        load_x(1)
+        wo_raw = keep.tile([P, PACK, C], BF16, name="wo_raw")
+        nc.sync.dma_start(out=wo_raw[:], in_=W_out.rearrange("(p j) w -> p j w", j=PACK))
+        bo = keep.tile([P, C], BF16, name="bo")
+        nc.sync.dma_start(out=bo[:], in_=b_out.partition_broadcast(P))
+        load_x(2)
+        load_kv(1)
+        load_x(3)
+        load_x(4)
+        load_x(5)
+
+        planes = {}
+        grouped = {}
+        xcodes = {}
+
+        def x_slice(k):
+            t0 = k * CHUNK
+            for start, width, t in x_tiles:
+                if start <= t0 < start + width:
+                    return t, t0 - start
+
+        def widen(k, j, eng):
+            if j == 0:
+                planes[k] = work.tile([P, PACK, CHUNK], BF16, name="planes", align_bytes=64)
+            t, off = x_slice(k)
+            src = t[:, j, off : off + CHUNK].bitcast(FP8)
+            dst = planes[k][:, j, :]
+            if eng == "s":
+                nc.scalar.activation(out=dst, in_=src, func=ACT.Copy, scale=xs[:, j : j + 1])
+            else:
+                nc.vector.tensor_scalar(out=dst, in0=src, scalar1=xs[:, j : j + 1], scalar2=None, op0=ALU.mult)
+
+        def interleave(k, part, parts, eng):
+            if part == 0:
+                grouped[k] = work.tile([P, CHUNK, PACK], BF16, name="grouped", align_bytes=64)
+            w = CHUNK // parts
+            dst = grouped[k][:, part * w : (part + 1) * w, :]
+            src = planes[k][:, :, part * w : (part + 1) * w].rearrange("p j w -> p w j")
+            if eng == "g":
+                nc.gpsimd.tensor_scalar(out=dst, in0=src, scalar1=1.0, scalar2=0.0, op0=ALU.mult, op1=ALU.add)
+            else:
+                nc.vector.tensor_copy(out=dst, in_=src)
+
+        def quantize_x(k):
+            codes = work.tile([P, CHUNK], U32, name="xcodes", align_bytes=64)
+            scales = work.tile([P, CHUNK], U8, name="xscales", align_bytes=64)
+            nc.vector.quantize_mx(out=codes[:].bitcast(FP8X4), scales=scales[:], in_=grouped[k][:].rearrange("p w j -> p (w j)"))
+            xcodes[k] = (codes, scales)
+
+        warm = keep.tile([P, 1], F32, name="warm")
+        nc.vector.memset(warm[:], 1.0)
+        nc.scalar.activation(out=warm[:], in_=warm[:], func=ACT.Sqrt)
+        ident = keep.tile([P, P], F32, name="ident", align_bytes=64)
+        make_identity(nc, ident[:])
+        ident_b = keep.tile([P, P], BF16, name="ident_b", align_bytes=64)
+        nc.vector.tensor_copy(out=ident_b[:], in_=ident[:])
+        sel = keep.tile([P, BLK], F32, name="sel")
+        nc.vector.tensor_reduce(out=sel[:], in_=ident[:].rearrange("p (i q) -> p i q", q=Q), axis=AXIS.X, op=ALU.add)
+        rows_k = keep.tile([P, 1], F32, name="rows_k")
+        nc.vector.tensor_reduce(out=rows_k[:], in_=ident[:].rearrange("p (i q) -> p i q", q=Q)[:, :, 0:3], axis=AXIS.XY, op=ALU.add)
+        rows_m = keep.tile([P, 1], F32, name="rows_m")
+        nc.vector.tensor_reduce(out=rows_m[:], in_=ident[:].rearrange("p (i q) -> p i q", q=Q)[:, :, 3:6], axis=AXIS.XY, op=ALU.add)
+        pieces = keep.tile([P, NTILES, Q], BF16, name="pieces", align_bytes=64)
+        nc.vector.memset(pieces[:], 0.0)
+
+        widen(0, 0, "s")
+        widen(0, 1, "s")
+        widen(0, 2, "v")
+        widen(0, 3, "v")
+        interleave(0, 0, 1, "v")
+        quantize_x(0)
+
+        wq_grouped = keep.tile([P, C, PACK], BF16, name="wq_grouped", align_bytes=64)
+        wq_codes = keep.tile([P, C], U32, name="wq_codes", align_bytes=64)
+        wq_scales = keep.tile([P, C], U8, name="wq_scales", align_bytes=64)
+        for u in range(2):
+            dst = wq_grouped[:, u * 256 : (u + 1) * 256, :].rearrange("p (m e) j -> p m e j", e=2)
+            src = wq_raw[:].rearrange("p j (m u e) -> p u m e j", u=2, e=2)[:, u]
+            if u == 0:
+                nc.vector.tensor_copy(out=dst, in_=src)
+            else:
+                nc.scalar.copy(out=dst, in_=src)
+        nc.vector.quantize_mx(out=wq_codes[:].bitcast(FP8X4), scales=wq_scales[:], in_=wq_grouped[:].rearrange("p w j -> p (w j)"))
+
+        for j in range(PACK):
+            widen(1, j, "s")
+        for i in range(4):
+            interleave(1, i, 4, "g")
+
+        wo_grouped = keep.tile([P, C, PACK], BF16, name="wo_grouped", align_bytes=64)
+        wo_codes = keep.tile([P, C], U32, name="wo_codes", align_bytes=64)
+        wo_scales = keep.tile([P, C], U8, name="wo_scales", align_bytes=64)
+        for i in range(4):
+            nc.gpsimd.tensor_scalar(
+                out=wo_grouped[:, i * 128 : (i + 1) * 128, :],
+                in0=wo_raw[:, :, i * 128 : (i + 1) * 128].rearrange("p j w -> p w j"),
+                scalar1=1.0, scalar2=0.0, op0=ALU.mult, op1=ALU.add,
+            )
+
+        q0 = {}
+        gate = {}
+        qb = {}
+        ss = {}
+        rn = {}
+        gt = {}
+        tr = {}
+        gw = {}
+        gcodes = {}
+        y_ps = {}
+
+        def mm1(k, i):
+            codes, scales = xcodes[k]
+            cols = slice(i * TILE, (i + 1) * TILE)
+            q0[k, i] = psum.tile([P, C], F32, name="q0")
+            nc.tensor.matmul_mx(out=q0[k, i][:], lhsT=codes[:, cols].bitcast(FP8X4), lhsT_scale=scales[:, cols],
+                                rhs=wq_codes[:].bitcast(FP8X4), rhs_scale=wq_scales[:], start=True, stop=True)
+
+        mm1(0, 0)
+        mm1(0, 1)
+
+        mrow32 = keep.tile([P, P], F32, name="mrow32", align_bytes=64)
+        nc.vector.tensor_copy(out=mrow32[:], in_=mrow[:])
+        m_ps = psum.tile([P, P], F32, name="m_ps", tag="tr")
+        nc.tensor.transpose(m_ps[:], mrow32[:], ident[:])
+        m = keep.tile([P, NTILES], F32, name="m")
+        nc.vector.tensor_copy(out=m[:], in_=m_ps[:, 0:NTILES])
+        sg = keep.tile([P, NTILES], F32, name="sg")
+        inv_sg = keep.tile([P, NTILES], F32, name="inv_sg")
+        m2 = keep.tile([P, NTILES], F32, name="m2")
+        v = keep.tile([P, 2, NTILES], F32, name="v")
+        pv = pieces[:, :, 0:6].rearrange("p i (v q) -> p v i q", q=3)
+        bq = keep.tile([P, C], BF16, name="bq")
+        nc.vector.tensor_scalar(out=sg[:], in0=m[:], scalar1=1.4, scalar2=-1.7, op0=ALU.mult, op1=ALU.add)
+        nc.vector.tensor_mul(out=m2[:], in0=m[:], in1=m[:])
+        nc.vector.tensor_mul(out=sg[:], in0=sg[:], in1=m[:])
+        nc.vector.tensor_copy(out=bq[:].rearrange("p (u m e) -> p u m e", u=2, e=2), in_=bq_raw[:].rearrange("p (m u e) -> p u m e", u=2, e=2))
+        nc.vector.tensor_scalar(out=sg[:], in0=sg[:], scalar1=1.0, scalar2=None, op0=ALU.add)
+
+        kv_rows = []
+        kvk = []
+        dkv = []
+
+        def prepare_kv(img):
+            perm = "p (m u e) -> p u m e"
+            a = keep.tile([P, C], BF16, name=f"kvk{img}")
+            b = keep.tile([P, C], BF16, name=f"kvm{img}")
+            nc.vector.tensor_copy(out=a[:].rearrange("p (u m e) -> p u m e", u=2, e=2), in_=kv_raw[img][0][:].rearrange(perm, u=2, e=2))
+            nc.vector.tensor_copy(out=b[:].rearrange("p (u m e) -> p u m e", u=2, e=2), in_=kv_raw[img][1][:].rearrange(perm, u=2, e=2))
+            r = keep.tile([P, C], BF16, name=f"kv_rows{img}", align_bytes=64)
+            d = keep.tile([P, C], F32, name=f"dkv{img}")
+            nc.vector.tensor_scalar(out=r[:], in0=a[:], scalar1=rows_k[:], scalar2=None, op0=ALU.mult)
+            nc.vector.tensor_sub(out=d[:], in0=b[:], in1=a[:])
+            nc.vector.scalar_tensor_tensor(out=r[:], in0=b[:], scalar=rows_m[:], in1=r[:], op0=ALU.mult, op1=ALU.add)
+            kv_rows.append(r)
+            kvk.append(a)
+            dkv.append(d)
+
+        nc.vector.reciprocal(out=inv_sg[:], in_=sg[:])
+        nc.vector.scalar_tensor_tensor(out=v[:, 1, :], in0=m2[:], scalar=0.7, in1=inv_sg[:], op0=ALU.mult, op1=ALU.mult)
+        nc.vector.tensor_scalar(out=v[:, 0, :], in0=v[:, 1, :], scalar1=-1.0, scalar2=1.0, op0=ALU.mult, op1=ALU.add)
+        res = v
+        for piece in range(3):
+            nc.vector.tensor_copy(out=pv[:, :, :, piece], in_=res[:])
+            if piece < 2:
+                nxt = keep.tile([P, 2, NTILES], F32, name=f"res{piece}")
+                nc.vector.tensor_sub(out=nxt[:], in0=res[:], in1=pv[:, :, :, piece])
+                res = nxt
+        pt_ps = psum.tile([P, 4, P], BF16, name="pt_ps", tag="tr")
+        for b in range(4):
+            nc.tensor.transpose(pt_ps[:, b, :], pieces[:, b * BLK : (b + 1) * BLK, :].rearrange("p i q -> p (i q)"), ident_b[:])
+        pt = keep.tile([P, 4, P], BF16, name="pt", align_bytes=64)
+        ptm = keep.tile([P, BLK, 4, P], BF16, name="ptm", align_bytes=64)
+
+        def mask_pieces(ii):
+            nc.vector.tensor_scalar(out=ptm[:, ii], in0=pt[:], scalar1=sel[:, ii : ii + 1], scalar2=None, op0=ALU.mult)
+
+        def sbuf_gated(k, i):
+            return i == NT - 1 and k >= FIRST_SBUF_GATE
+
+        def make_gate(k, i):
+            t = k * NT + i
+            img = k // PER_IMG
+            gate[k, i] = psum.tile([P, C], F32, name="gate")
+            nc.tensor.matmul(gate[k, i][:], lhsT=ptm[:, t % BLK, t // BLK, :], rhs=kv_rows[img][:], start=True, stop=True)
+
+        def make_gate_sbuf(k, i):
+            t = k * NT + i
+            img = k // PER_IMG
+            gate[k, i] = work.tile([P, C], F32, name="gate_sb", bufs=2)
+            nc.vector.scalar_tensor_tensor(out=gate[k, i][:], in0=dkv[img][:], scalar=v[:, 1, t : t + 1], in1=kvk[img][:], op0=ALU.mult, op1=ALU.add)
+
+        def add_bias(k, i):
+            qb[k, i] = work.tile([P, C], F32, name="qb", bufs=10)
+            nc.vector.tensor_add(out=qb[k, i][:], in0=q0.pop((k, i))[:], in1=bq[:])
+
+        def squares(k, i):
+            if i == 0:
+                ss[k] = work.tile([P, NT], F32, name="ss")
+            t = k * NT + i
+            junk = work.tile([P, C], BF16, name="junk", bufs=2)
+            nc.scalar.activation(out=junk[:], in_=qb[k, i][:], func=ACT.Square, scale=inv_sg[:, t : t + 1], accum_out=ss[k][:, i : i + 1])
+
+        def root(k):
+            nc.scalar.activation(out=ss[k][:], in_=ss[k][:], func=ACT.Sqrt)
+
+        def recip(k):
+            rn[k] = work.tile([P, NT], F32, name="rn")
+            nc.vector.reciprocal(out=rn[k][:], in_=ss[k][:])
+
+        def gating(k, i):
+            gt[k, i] = work.tile([P, C], BF16, name="gt", bufs=6, align_bytes=64)
+            nc.vector.scalar_tensor_tensor(out=gt[k, i][:], in0=gate.pop((k, i))[:], scalar=rn[k][:, i : i + 1], in1=qb.pop((k, i))[:], op0=ALU.mult, op1=ALU.mult)
+
+        def turn(k, h):
+            tr[k, h] = psum.tile([P, 2, 2, TILE], F32, name="tr", tag="tr")
+            for a in range(2):
+                words = gt.pop((k, 2 * h + a))[:].bitcast(F32)
+                for u in range(2):
+                    nc.tensor.transpose(tr[k, h][:, a, u, :], words[:, u * 128 : (u + 1) * 128], ident[:])
+
+        def unload(k, h):
+            if h == 0:
+                gw[k] = work.tile([P, CHUNK, PACK], BF16, name="gw", align_bytes=64)
+            dst = gw[k][:].rearrange("p w j -> p (w j)").bitcast(F32)[:, h * 512 : (h + 1) * 512]
+            nc.scalar.copy(out=dst.rearrange("p (a r u) -> p a r u", a=2, u=2), in_=tr.pop((k, h))[:].rearrange("p a u r -> p a r u"))
+
+        def quantize_g(k):
+            codes = work.tile([P, CHUNK], U32, name="gcodes", align_bytes=64)
+            scales = work.tile([P, CHUNK], U8, name="gscales", align_bytes=64)
+            nc.vector.quantize_mx(out=codes[:].bitcast(FP8X4), scales=scales[:], in_=gw.pop(k)[:].rearrange("p w j -> p (w j)"))
+            gcodes[k] = (codes, scales)
+
+        def mm2(k, i):
+            codes, scales = gcodes[k]
+            cols = slice(i * TILE, (i + 1) * TILE)
+            y_ps[k, i] = psum.tile([P, C], F32, name="y_ps")
+            nc.tensor.matmul_mx(out=y_ps[k, i][:], lhsT=codes[:, cols].bitcast(FP8X4), lhsT_scale=scales[:, cols],
+                                rhs=wo_codes[:].bitcast(FP8X4), rhs_scale=wo_scales[:], start=True, stop=True)
+
+        def finish(k, i, eng):
+            y = work.tile([P, C], F32, name="y", bufs=8)
+            src = y_ps.pop((k, i))
+            if eng == "v":
+                nc.vector.tensor_add(out=y[:], in0=src[:], in1=bo[:])
+            else:
+                nc.scalar.copy(out=y[:], in_=src[:])
+                nc.gpsimd.tensor_add(out=y[:], in0=y[:], in1=bo[:])
+            t = k * NT + i
+            nc.sync.dma_start(out=out_rows[t * TILE : (t + 1) * TILE, :], in_=y[:])
+
+        def step(s):
+            new = s < NCHUNKS
+            mid = 0 <= s - 1 < NCHUNKS
+            old = 0 <= s - 2 < NCHUNKS
+            if mid:
+                root(s - 1)
+            if new:
+                add_bias(s, 0)
+                mm1(s, 2)
+            if s == 0:
+                nc.vector.tensor_copy(out=pt[:], in_=pt_ps[:])
+                prepare_kv(0)
+            if s < 4:
+                for ii in range(4 * s, 4 * s + 4):
+                    mask_pieces(ii)
+            if old:
+                unload(s - 2, 1)
+            if s + 2 < NCHUNKS:
+                interleave(s + 2, 0, 4, "g")
+                interleave(s + 2, 1, 4, "g")
+            if new:
+                squares(s, 0)
+            if s + 3 < NCHUNKS:
+                widen(s + 3, 0, "s")
+            if mid:
+                recip(s - 1)
+                gating(s - 1, 0)
+                make_gate(s - 1, 2)
+            if new:
+                add_bias(s, 1)
+                squares(s, 1)
+                mm1(s, 3)
+            if s + 3 < NCHUNKS:
+                widen(s + 3, 1, "s")
+            if mid:
+                gating(s - 1, 1)
+                if not sbuf_gated(s - 1, 3):
+                    make_gate(s - 1, 3)
+                turn(s - 1, 0)
+                unload(s - 1, 0)
+            if old:
+                if s == 2:
+                    nc.vector.quantize_mx(out=wo_codes[:].bitcast(FP8X4), scales=wo_scales[:], in_=wo_grouped[:].rearrange("p w j -> p (w j)"))
+                quantize_g(s - 2)
+                mm2(s - 2, 0)
+                mm2(s - 2, 1)
+                finish(s - 2, 0, "s")
+                mm2(s - 2, 2)
+            if s + 1 < NCHUNKS:
+                quantize_x(s + 1)
+            if s == 3:
+                prepare_kv(1)
+            if new:
+                add_bias(s, 2)
+                squares(s, 2)
+            if s + 2 < NCHUNKS:
+                interleave(s + 2, 2, 4, "g")
+            if s + 3 < NCHUNKS:
+                widen(s + 3, 2, "s")
+            if s + 1 < NCHUNKS:
+                mm1(s + 1, 0)
+            if old:
+                finish(s - 2, 1, "v")
+                mm2(s - 2, 3)
+            if mid:
+                gating(s - 1, 2)
+            if new:
+                make_gate(s, 0)
+            if old:
+                finish(s - 2, 2, "s")
+            if s + 2 < NCHUNKS:
+                interleave(s + 2, 3, 4, "g")
+            if mid and sbuf_gated(s - 1, 3):
+                make_gate_sbuf(s - 1, 3)
+            if new:
+                add_bias(s, 3)
+                squares(s, 3)
+            if s + 1 < NCHUNKS:
+                mm1(s + 1, 1)
+            if s + 3 < NCHUNKS:
+                widen(s + 3, 3, "s")
+            if mid:
+                gating(s - 1, 3)
+                turn(s - 1, 1)
+            if new:
+                make_gate(s, 1)
+            if old:
+                finish(s - 2, 3, "v")
+
+        for j in range(PACK):
+            widen(2, j, "s")
+        for s in range(NCHUNKS + 2):
+            step(s)

@@ -30,7 +30,10 @@ Q = 8
 FLOPS = 2 * 2 * B * N * C * C
 
 X_LOADS = ((0, 0, 512), (0, 512, 512), (0, 1024, 1024), (0, 2048, 2048), (1, 0, 2048), (1, 2048, 2048))
-FIRST_SBUF_GATE = 3
+FIRST_TURNED_GATE = 3
+COLUMNS = {2: 0, 5: 1}
+MASKS = {1: range(10, 14), 2: range(14, 16)}
+A1 = "v"
 
 
 def tile_hydraattention_pb_t_kernel(tc, x_bytes, x_scale, mask, W_q, b_q, kv_know, kv_mask, W_out, b_out, out):
@@ -43,6 +46,9 @@ def tile_hydraattention_pb_t_kernel(tc, x_bytes, x_scale, mask, W_q, b_q, kv_kno
         psum = ctx.enter_context(tc.psum_pool(name="psum", bufs=2))
         ctx.enter_context(tc.manual_schedule())
 
+        mrow = keep.tile([P, P], BF16, name="mrow")
+        nc.vector.memset(mrow[:], 0.0)
+        nc.sync.dma_start(out=mrow[0:NTILES, :], in_=mask.rearrange("b o (r q) w -> (b o r) (q w)", q=2))
         xs = keep.tile([P, PACK], F32, name="xs")
         nc.sync.dma_start(out=xs[:], in_=x_scale.rearrange("o (p j) a b -> p (o j a b)", j=PACK))
         x_tiles = []
@@ -56,11 +62,9 @@ def tile_hydraattention_pb_t_kernel(tc, x_bytes, x_scale, mask, W_q, b_q, kv_kno
         load_x(0)
         wq_raw = keep.tile([P, PACK, C], BF16, name="wq_raw")
         nc.sync.dma_start(out=wq_raw[:], in_=W_q.rearrange("(p j) w -> p j w", j=PACK))
-        mrow = keep.tile([P, P], BF16, name="mrow")
-        nc.vector.memset(mrow[:], 0.0)
-        nc.sync.dma_start(out=mrow[0:NTILES, :], in_=mask.rearrange("b o (r q) w -> (b o r) (q w)", q=2))
         bq_raw = keep.tile([P, C], BF16, name="bq_raw")
         nc.sync.dma_start(out=bq_raw[:], in_=b_q.partition_broadcast(P))
+        load_x(1)
         kv_raw = []
 
         def load_kv(img):
@@ -71,54 +75,67 @@ def tile_hydraattention_pb_t_kernel(tc, x_bytes, x_scale, mask, W_q, b_q, kv_kno
             kv_raw.append((a, b))
 
         load_kv(0)
-        load_x(1)
+        load_x(2)
         wo_raw = keep.tile([P, PACK, C], BF16, name="wo_raw")
         nc.sync.dma_start(out=wo_raw[:], in_=W_out.rearrange("(p j) w -> p j w", j=PACK))
         bo = keep.tile([P, C], BF16, name="bo")
         nc.sync.dma_start(out=bo[:], in_=b_out.partition_broadcast(P))
-        load_x(2)
         load_kv(1)
         load_x(3)
         load_x(4)
         load_x(5)
 
         planes = {}
-        grouped = {}
         xcodes = {}
+        gcodes = {}
+        batch = {}
 
-        def x_slice(k):
+        def widen(k, chunks, j, eng):
             t0 = k * CHUNK
+            w = chunks * CHUNK
+            if j == 0:
+                pl = work.tile([P, PACK, 2 * CHUNK], BF16, name="planes", align_bytes=64)
+                for c in range(chunks):
+                    planes[k + c] = pl[:, :, c * CHUNK : (c + 1) * CHUNK]
+                planes["w", k] = pl
             for start, width, t in x_tiles:
                 if start <= t0 < start + width:
-                    return t, t0 - start
-
-        def widen(k, j, eng):
-            if j == 0:
-                planes[k] = work.tile([P, PACK, CHUNK], BF16, name="planes", align_bytes=64)
-            t, off = x_slice(k)
-            src = t[:, j, off : off + CHUNK].bitcast(FP8)
-            dst = planes[k][:, j, :]
+                    src = t[:, j, t0 - start : t0 - start + w].bitcast(FP8)
+            dst = planes["w", k][:, j, 0:w]
             if eng == "s":
                 nc.scalar.activation(out=dst, in_=src, func=ACT.Copy, scale=xs[:, j : j + 1])
             else:
                 nc.vector.tensor_scalar(out=dst, in0=src, scalar1=xs[:, j : j + 1], scalar2=None, op0=ALU.mult)
 
+        def batch_half(s, half):
+            if s not in batch:
+                batch[s] = work.tile([P, 2, CHUNK, PACK], BF16, name="batch", align_bytes=64)
+            return batch[s][:, half]
+
         def interleave(k, part, parts, eng):
-            if part == 0:
-                grouped[k] = work.tile([P, CHUNK, PACK], BF16, name="grouped", align_bytes=64)
+            dst_all = batch_half(k - 1, 0)
             w = CHUNK // parts
-            dst = grouped[k][:, part * w : (part + 1) * w, :]
+            dst = dst_all[:, part * w : (part + 1) * w, :]
             src = planes[k][:, :, part * w : (part + 1) * w].rearrange("p j w -> p w j")
             if eng == "g":
                 nc.gpsimd.tensor_scalar(out=dst, in0=src, scalar1=1.0, scalar2=0.0, op0=ALU.mult, op1=ALU.add)
             else:
                 nc.vector.tensor_copy(out=dst, in_=src)
 
-        def quantize_x(k):
-            codes = work.tile([P, CHUNK], U32, name="xcodes", align_bytes=64)
-            scales = work.tile([P, CHUNK], U8, name="xscales", align_bytes=64)
-            nc.vector.quantize_mx(out=codes[:].bitcast(FP8X4), scales=scales[:], in_=grouped[k][:].rearrange("p w j -> p (w j)"))
-            xcodes[k] = (codes, scales)
+        def quantize(s):
+            lo = 0 if s + 1 < NCHUNKS else 1
+            hi = 2 if s - 2 >= 0 else 1
+            codes = work.tile([P, 2, CHUNK], U32, name="codes", align_bytes=64)
+            scales = work.tile([P, 2, CHUNK], U8, name="scales", align_bytes=64)
+            nc.vector.quantize_mx(
+                out=codes[:, lo:hi].rearrange("p h w -> p (h w)").bitcast(FP8X4),
+                scales=scales[:, lo:hi].rearrange("p h w -> p (h w)"),
+                in_=batch.pop(s)[:, lo:hi].rearrange("p h w j -> p (h w j)"),
+            )
+            if lo == 0:
+                xcodes[s + 1] = (codes[:, 0], scales[:, 0])
+            if hi == 2:
+                gcodes[s - 2] = (codes[:, 1], scales[:, 1])
 
         warm = keep.tile([P, 1], F32, name="warm")
         nc.vector.memset(warm[:], 1.0)
@@ -127,48 +144,74 @@ def tile_hydraattention_pb_t_kernel(tc, x_bytes, x_scale, mask, W_q, b_q, kv_kno
         make_identity(nc, ident[:])
         ident_b = keep.tile([P, P], BF16, name="ident_b", align_bytes=64)
         nc.vector.tensor_copy(out=ident_b[:], in_=ident[:])
+        by_tile = ident[:].rearrange("p (i q) -> p i q", q=Q)
         sel = keep.tile([P, BLK], F32, name="sel")
-        nc.vector.tensor_reduce(out=sel[:], in_=ident[:].rearrange("p (i q) -> p i q", q=Q), axis=AXIS.X, op=ALU.add)
+        nc.vector.tensor_reduce(out=sel[:], in_=by_tile, axis=AXIS.X, op=ALU.add)
         rows_k = keep.tile([P, 1], F32, name="rows_k")
-        nc.vector.tensor_reduce(out=rows_k[:], in_=ident[:].rearrange("p (i q) -> p i q", q=Q)[:, :, 0:3], axis=AXIS.XY, op=ALU.add)
+        nc.vector.tensor_reduce(out=rows_k[:], in_=by_tile[:, :, 0:3], axis=AXIS.XY, op=ALU.add)
         rows_m = keep.tile([P, 1], F32, name="rows_m")
-        nc.vector.tensor_reduce(out=rows_m[:], in_=ident[:].rearrange("p (i q) -> p i q", q=Q)[:, :, 3:6], axis=AXIS.XY, op=ALU.add)
+        nc.vector.tensor_reduce(out=rows_m[:], in_=by_tile[:, :, 3:6], axis=AXIS.XY, op=ALU.add)
         pieces = keep.tile([P, NTILES, Q], BF16, name="pieces", align_bytes=64)
         nc.vector.memset(pieces[:], 0.0)
 
-        widen(0, 0, "s")
-        widen(0, 1, "s")
-        widen(0, 2, "v")
-        widen(0, 3, "v")
+        mrow32 = keep.tile([P, P], F32, name="mrow32", align_bytes=64)
+        nc.vector.tensor_copy(out=mrow32[:], in_=mrow[:])
+        m_ps = psum.tile([P, P], F32, name="m_ps", tag="tr")
+        nc.tensor.transpose(m_ps[:], mrow32[:], ident[:])
+        m = keep.tile([P, NTILES], F32, name="m")
+        nc.scalar.copy(out=m[:], in_=m_ps[:, 0:NTILES])
+        t1 = keep.tile([P, NTILES], F32, name="t1")
+        t2 = keep.tile([P, NTILES], F32, name="t2")
+        t3 = keep.tile([P, NTILES], F32, name="t3")
+        t4 = keep.tile([P, NTILES], F32, name="t4")
+        sg = keep.tile([P, NTILES], F32, name="sg")
+        inv_sg = keep.tile([P, NTILES], F32, name="inv_sg")
+        v = keep.tile([P, 2, NTILES], F32, name="v")
+        pv = pieces[:, :, 0:6].rearrange("p i (v q) -> p v i q", q=3)
+        rest = [keep.tile([P, 2, NTILES], F32, name=f"rest{i}") for i in range(2)]
+
+        def g_affine(dst, src, a, b):
+            nc.gpsimd.tensor_scalar(out=dst, in0=src, scalar1=a, scalar2=b, op0=ALU.mult, op1=ALU.add)
+
+        g_affine(t1[:], m[:], 1.4, -1.7)
+        g_affine(t3[:], m[:], 0.7, 0.0)
+        nc.gpsimd.tensor_mul(out=t2[:], in0=t1[:], in1=m[:])
+        nc.gpsimd.tensor_mul(out=t4[:], in0=t3[:], in1=m[:])
+        g_affine(sg[:], t2[:], 1.0, 1.0)
+
+        widen(0, 1, 0, "s")
+        widen(0, 1, 1, "v")
+        widen(0, 1, 2, "v")
+        widen(0, 1, 3, "v")
+        nc.vector.reciprocal(out=inv_sg[:], in_=sg[:])
         interleave(0, 0, 1, "v")
-        quantize_x(0)
 
         wq_grouped = keep.tile([P, C, PACK], BF16, name="wq_grouped", align_bytes=64)
         wq_codes = keep.tile([P, C], U32, name="wq_codes", align_bytes=64)
         wq_scales = keep.tile([P, C], U8, name="wq_scales", align_bytes=64)
-        for u in range(2):
+
+        def permute_wq(u, eng):
             dst = wq_grouped[:, u * 256 : (u + 1) * 256, :].rearrange("p (m e) j -> p m e j", e=2)
             src = wq_raw[:].rearrange("p j (m u e) -> p u m e j", u=2, e=2)[:, u]
-            if u == 0:
-                nc.vector.tensor_copy(out=dst, in_=src)
+            if eng == "g":
+                g_affine(dst, src, 1.0, 0.0)
             else:
                 nc.scalar.copy(out=dst, in_=src)
+
+        permute_wq(1, "s")
+        permute_wq(0, "g")
+        nc.gpsimd.tensor_mul(out=v[:, 1, :], in0=t4[:], in1=inv_sg[:])
+        quantize(-1)
         nc.vector.quantize_mx(out=wq_codes[:].bitcast(FP8X4), scales=wq_scales[:], in_=wq_grouped[:].rearrange("p w j -> p (w j)"))
+        bq = keep.tile([P, C], BF16, name="bq")
+        nc.scalar.copy(out=bq[:].rearrange("p (u m e) -> p u m e", u=2, e=2), in_=bq_raw[:].rearrange("p (m u e) -> p u m e", u=2, e=2))
 
-        for j in range(PACK):
-            widen(1, j, "s")
-        for i in range(4):
-            interleave(1, i, 4, "g")
-
-        wo_grouped = keep.tile([P, C, PACK], BF16, name="wo_grouped", align_bytes=64)
-        wo_codes = keep.tile([P, C], U32, name="wo_codes", align_bytes=64)
-        wo_scales = keep.tile([P, C], U8, name="wo_scales", align_bytes=64)
-        for i in range(4):
-            nc.gpsimd.tensor_scalar(
-                out=wo_grouped[:, i * 128 : (i + 1) * 128, :],
-                in0=wo_raw[:, :, i * 128 : (i + 1) * 128].rearrange("p j w -> p w j"),
-                scalar1=1.0, scalar2=0.0, op0=ALU.mult, op1=ALU.add,
-            )
+        g_affine(v[:, 0, :], v[:, 1, :], -1.0, 1.0)
+        g_affine(pv[:, :, :, 0], v[:], 1.0, 0.0)
+        nc.gpsimd.tensor_sub(out=rest[0][:], in0=v[:], in1=pv[:, :, :, 0])
+        g_affine(pv[:, :, :, 1], rest[0][:], 1.0, 0.0)
+        nc.gpsimd.tensor_sub(out=rest[1][:], in0=rest[0][:], in1=pv[:, :, :, 1])
+        g_affine(pv[:, :, :, 2], rest[1][:], 1.0, 0.0)
 
         q0 = {}
         gate = {}
@@ -177,8 +220,6 @@ def tile_hydraattention_pb_t_kernel(tc, x_bytes, x_scale, mask, W_q, b_q, kv_kno
         rn = {}
         gt = {}
         tr = {}
-        gw = {}
-        gcodes = {}
         y_ps = {}
 
         def mm1(k, i):
@@ -191,76 +232,98 @@ def tile_hydraattention_pb_t_kernel(tc, x_bytes, x_scale, mask, W_q, b_q, kv_kno
         mm1(0, 0)
         mm1(0, 1)
 
-        mrow32 = keep.tile([P, P], F32, name="mrow32", align_bytes=64)
-        nc.vector.tensor_copy(out=mrow32[:], in_=mrow[:])
-        m_ps = psum.tile([P, P], F32, name="m_ps", tag="tr")
-        nc.tensor.transpose(m_ps[:], mrow32[:], ident[:])
-        m = keep.tile([P, NTILES], F32, name="m")
-        nc.vector.tensor_copy(out=m[:], in_=m_ps[:, 0:NTILES])
-        sg = keep.tile([P, NTILES], F32, name="sg")
-        inv_sg = keep.tile([P, NTILES], F32, name="inv_sg")
-        m2 = keep.tile([P, NTILES], F32, name="m2")
-        v = keep.tile([P, 2, NTILES], F32, name="v")
-        pv = pieces[:, :, 0:6].rearrange("p i (v q) -> p v i q", q=3)
-        bq = keep.tile([P, C], BF16, name="bq")
-        nc.vector.tensor_scalar(out=sg[:], in0=m[:], scalar1=1.4, scalar2=-1.7, op0=ALU.mult, op1=ALU.add)
-        nc.vector.tensor_mul(out=m2[:], in0=m[:], in1=m[:])
-        nc.vector.tensor_mul(out=sg[:], in0=sg[:], in1=m[:])
-        nc.vector.tensor_copy(out=bq[:].rearrange("p (u m e) -> p u m e", u=2, e=2), in_=bq_raw[:].rearrange("p (m u e) -> p u m e", u=2, e=2))
-        nc.vector.tensor_scalar(out=sg[:], in0=sg[:], scalar1=1.0, scalar2=None, op0=ALU.add)
-
-        kv_rows = []
-        kvk = []
-        dkv = []
-
-        def prepare_kv(img):
-            perm = "p (m u e) -> p u m e"
-            a = keep.tile([P, C], BF16, name=f"kvk{img}")
-            b = keep.tile([P, C], BF16, name=f"kvm{img}")
-            nc.vector.tensor_copy(out=a[:].rearrange("p (u m e) -> p u m e", u=2, e=2), in_=kv_raw[img][0][:].rearrange(perm, u=2, e=2))
-            nc.vector.tensor_copy(out=b[:].rearrange("p (u m e) -> p u m e", u=2, e=2), in_=kv_raw[img][1][:].rearrange(perm, u=2, e=2))
-            r = keep.tile([P, C], BF16, name=f"kv_rows{img}", align_bytes=64)
-            d = keep.tile([P, C], F32, name=f"dkv{img}")
-            nc.vector.tensor_scalar(out=r[:], in0=a[:], scalar1=rows_k[:], scalar2=None, op0=ALU.mult)
-            nc.vector.tensor_sub(out=d[:], in0=b[:], in1=a[:])
-            nc.vector.scalar_tensor_tensor(out=r[:], in0=b[:], scalar=rows_m[:], in1=r[:], op0=ALU.mult, op1=ALU.add)
-            kv_rows.append(r)
-            kvk.append(a)
-            dkv.append(d)
-
-        nc.vector.reciprocal(out=inv_sg[:], in_=sg[:])
-        nc.vector.scalar_tensor_tensor(out=v[:, 1, :], in0=m2[:], scalar=0.7, in1=inv_sg[:], op0=ALU.mult, op1=ALU.mult)
-        nc.vector.tensor_scalar(out=v[:, 0, :], in0=v[:, 1, :], scalar1=-1.0, scalar2=1.0, op0=ALU.mult, op1=ALU.add)
-        res = v
-        for piece in range(3):
-            nc.vector.tensor_copy(out=pv[:, :, :, piece], in_=res[:])
-            if piece < 2:
-                nxt = keep.tile([P, 2, NTILES], F32, name=f"res{piece}")
-                nc.vector.tensor_sub(out=nxt[:], in0=res[:], in1=pv[:, :, :, piece])
-                res = nxt
+        pt = keep.tile([P, 4, P], BF16, name="pt", align_bytes=64)
+        ptm = keep.tile([P, BLK, 4, P], BF16, name="ptm", align_bytes=64)
         pt_ps = psum.tile([P, 4, P], BF16, name="pt_ps", tag="tr")
         for b in range(4):
             nc.tensor.transpose(pt_ps[:, b, :], pieces[:, b * BLK : (b + 1) * BLK, :].rearrange("p i q -> p (i q)"), ident_b[:])
-        pt = keep.tile([P, 4, P], BF16, name="pt", align_bytes=64)
-        ptm = keep.tile([P, BLK, 4, P], BF16, name="ptm", align_bytes=64)
 
-        def mask_pieces(ii):
-            nc.vector.tensor_scalar(out=ptm[:, ii], in0=pt[:], scalar1=sel[:, ii : ii + 1], scalar2=None, op0=ALU.mult)
+        def mask_pieces(ii, eng):
+            eng.tensor_scalar(out=ptm[:, ii], in0=pt[:], scalar1=sel[:, ii : ii + 1], scalar2=1.0, op0=ALU.mult, op1=ALU.mult)
 
-        def sbuf_gated(k, i):
-            return i == NT - 1 and k >= FIRST_SBUF_GATE
+        for j in range(PACK):
+            widen(1, 1, j, A1)
+        for i in range(4):
+            interleave(1, i, 4, "g")
+
+        widen(2, 2, 0, "s")
+        widen(2, 2, 1, "s")
+
+        kv_rows = []
+        kcol = []
+        dcol = []
+
+        def prepare_kv(img, eng):
+            parts = []
+            for raw, rows, nm in ((kv_raw[img][0], rows_k, "a"), (kv_raw[img][1], rows_m, "b")):
+                r = keep.tile([P, C], BF16, name=f"kv_{nm}{img}")
+                eng.tensor_scalar(out=r[:].rearrange("p (u m e) -> p u m e", u=2, e=2), in0=raw[:].rearrange("p (m u e) -> p u m e", u=2, e=2),
+                                  scalar1=rows[:], scalar2=1.0, op0=ALU.mult, op1=ALU.mult)
+                parts.append(r)
+            r = keep.tile([P, C], BF16, name=f"kv_rows{img}", align_bytes=64)
+            eng.tensor_add(out=r[:], in0=parts[0][:], in1=parts[1][:])
+            kv_rows.append(r)
+
+        col_ps = {}
+
+        def turn_columns(img):
+            col_ps[img] = psum.tile([P, 4, P], BF16, name="kv_ps", tag="tr")
+            for r in range(4):
+                nc.tensor.transpose(col_ps[img][:, r, :], kv_rows[img][:, r * P : (r + 1) * P], ident_b[:])
+
+        def take_columns(img):
+            k = keep.tile([P, 4], F32, name=f"kcol{img}")
+            d = keep.tile([P, 4], F32, name=f"dcol{img}")
+            ps = col_ps.pop(img)
+            nc.vector.tensor_copy(out=k[:], in_=ps[:, :, 0])
+            nc.vector.tensor_sub(out=d[:], in0=ps[:, :, 3], in1=k[:])
+            kcol.append(k)
+            dcol.append(d)
+
+        n_tg = NCHUNKS - FIRST_TURNED_GATE
+        rho_bc = keep.tile([P, n_tg, TILE], F32, name="rho_bc", align_bytes=64)
+
+        def spread_rho(a):
+            n = min(4, n_tg - a)
+            ps = psum.tile([P, 4, TILE], F32, name="rho_ps", tag="tr")
+            for i in range(n):
+                t = (FIRST_TURNED_GATE + a + i) * NT + NT - 1
+                nc.tensor.transpose(ps[:, i, :], v[:, 1, t : t + 1].to_broadcast([P, P]), ident[:])
+            nc.scalar.copy(out=rho_bc[:, a : a + n, :], in_=ps[:, 0:n, :])
+
+        wo_grouped = keep.tile([P, C, PACK], BF16, name="wo_grouped", align_bytes=64)
+        wo_codes = keep.tile([P, C], U32, name="wo_codes", align_bytes=64)
+        wo_scales = keep.tile([P, C], U8, name="wo_scales", align_bytes=64)
+
+        def interleave_wo(i):
+            nc.gpsimd.tensor_scalar(
+                out=wo_grouped[:, i * 128 : (i + 1) * 128, :],
+                in0=wo_raw[:, :, i * 128 : (i + 1) * 128].rearrange("p j w -> p w j"),
+                scalar1=1.0, scalar2=0.0, op0=ALU.mult, op1=ALU.add,
+            )
+
+        def turned(k, i):
+            return i == NT - 1 and k >= FIRST_TURNED_GATE
+
+        gate_t = {}
+
+        def gate_columns(k):
+            img = k // PER_IMG
+            gate_t[k] = work.tile([P, 4, TILE], F32, name="gate_t", align_bytes=64)
+            for r in range(4):
+                nc.gpsimd.tensor_scalar(out=gate_t[k][:, r, :], in0=rho_bc[:, k - FIRST_TURNED_GATE, :], scalar1=dcol[img][:, r : r + 1],
+                                        scalar2=kcol[img][:, r : r + 1], op0=ALU.mult, op1=ALU.add)
 
         def make_gate(k, i):
             t = k * NT + i
             img = k // PER_IMG
             gate[k, i] = psum.tile([P, C], F32, name="gate")
-            nc.tensor.matmul(gate[k, i][:], lhsT=ptm[:, t % BLK, t // BLK, :], rhs=kv_rows[img][:], start=True, stop=True)
-
-        def make_gate_sbuf(k, i):
-            t = k * NT + i
-            img = k // PER_IMG
-            gate[k, i] = work.tile([P, C], F32, name="gate_sb", bufs=2)
-            nc.vector.scalar_tensor_tensor(out=gate[k, i][:], in0=dkv[img][:], scalar=v[:, 1, t : t + 1], in1=kvk[img][:], op0=ALU.mult, op1=ALU.add)
+            if turned(k, i):
+                g = gate_t.pop(k)
+                for r in range(4):
+                    nc.tensor.transpose(gate[k, i][:, r * P : (r + 1) * P], g[:, r, :], ident[:])
+            else:
+                nc.tensor.matmul(gate[k, i][:], lhsT=ptm[:, t % BLK, t // BLK, :], rhs=kv_rows[img][:], start=True, stop=True)
 
         def add_bias(k, i):
             qb[k, i] = work.tile([P, C], F32, name="qb", bufs=10)
@@ -292,16 +355,8 @@ def tile_hydraattention_pb_t_kernel(tc, x_bytes, x_scale, mask, W_q, b_q, kv_kno
                     nc.tensor.transpose(tr[k, h][:, a, u, :], words[:, u * 128 : (u + 1) * 128], ident[:])
 
         def unload(k, h):
-            if h == 0:
-                gw[k] = work.tile([P, CHUNK, PACK], BF16, name="gw", align_bytes=64)
-            dst = gw[k][:].rearrange("p w j -> p (w j)").bitcast(F32)[:, h * 512 : (h + 1) * 512]
+            dst = batch_half(k + 2, 1).rearrange("p w j -> p (w j)").bitcast(F32)[:, h * 512 : (h + 1) * 512]
             nc.scalar.copy(out=dst.rearrange("p (a r u) -> p a r u", a=2, u=2), in_=tr.pop((k, h))[:].rearrange("p a u r -> p a r u"))
-
-        def quantize_g(k):
-            codes = work.tile([P, CHUNK], U32, name="gcodes", align_bytes=64)
-            scales = work.tile([P, CHUNK], U8, name="gscales", align_bytes=64)
-            nc.vector.quantize_mx(out=codes[:].bitcast(FP8X4), scales=scales[:], in_=gw.pop(k)[:].rearrange("p w j -> p (w j)"))
-            gcodes[k] = (codes, scales)
 
         def mm2(k, i):
             codes, scales = gcodes[k]
@@ -321,30 +376,34 @@ def tile_hydraattention_pb_t_kernel(tc, x_bytes, x_scale, mask, W_q, b_q, kv_kno
             t = k * NT + i
             nc.sync.dma_start(out=out_rows[t * TILE : (t + 1) * TILE, :], in_=y[:])
 
+        def widen_jobs(s):
+            if s < 2:
+                return [(2, 2), (2, 3), (4, 0)] if s == 0 else [(4, 1), (4, 2), (4, 3)]
+            pair = s + 4 - s % 2
+            return [(pair, 2 * (s % 2) + i) for i in range(2)] if pair < NCHUNKS else []
+
         def step(s):
             new = s < NCHUNKS
             mid = 0 <= s - 1 < NCHUNKS
             old = 0 <= s - 2 < NCHUNKS
-            if mid:
-                root(s - 1)
+            jobs = widen_jobs(s)
+            fill = s + 2 < NCHUNKS
             if new:
                 add_bias(s, 0)
                 mm1(s, 2)
+            if s - 1 in COLUMNS:
+                take_columns(COLUMNS[s - 1])
             if s == 0:
                 nc.vector.tensor_copy(out=pt[:], in_=pt_ps[:])
-                prepare_kv(0)
-            if s < 4:
-                for ii in range(4 * s, 4 * s + 4):
-                    mask_pieces(ii)
             if old:
                 unload(s - 2, 1)
-            if s + 2 < NCHUNKS:
+            if fill and s > 0:
                 interleave(s + 2, 0, 4, "g")
                 interleave(s + 2, 1, 4, "g")
             if new:
                 squares(s, 0)
-            if s + 3 < NCHUNKS:
-                widen(s + 3, 0, "s")
+            for k, j in jobs[0:1]:
+                widen(k, 2, j, "s")
             if mid:
                 recip(s - 1)
                 gating(s - 1, 0)
@@ -353,55 +412,70 @@ def tile_hydraattention_pb_t_kernel(tc, x_bytes, x_scale, mask, W_q, b_q, kv_kno
                 add_bias(s, 1)
                 squares(s, 1)
                 mm1(s, 3)
-            if s + 3 < NCHUNKS:
-                widen(s + 3, 1, "s")
+            for k, j in jobs[2:3]:
+                widen(k, 2, j, "s")
+            if s == 0:
+                prepare_kv(0, nc.vector)
+                for ii in range(4):
+                    mask_pieces(ii, nc.vector)
             if mid:
                 gating(s - 1, 1)
-                if not sbuf_gated(s - 1, 3):
-                    make_gate(s - 1, 3)
                 turn(s - 1, 0)
+                make_gate(s - 1, 3)
                 unload(s - 1, 0)
+            if s == 1:
+                interleave(2, 1, 2, "v")
+            if s == 2:
+                nc.vector.quantize_mx(out=wo_codes[:].bitcast(FP8X4), scales=wo_scales[:], in_=wo_grouped[:].rearrange("p w j -> p (w j)"))
+            if s + 1 < NCHUNKS or old:
+                quantize(s)
             if old:
-                if s == 2:
-                    nc.vector.quantize_mx(out=wo_codes[:].bitcast(FP8X4), scales=wo_scales[:], in_=wo_grouped[:].rearrange("p w j -> p (w j)"))
-                quantize_g(s - 2)
                 mm2(s - 2, 0)
                 mm2(s - 2, 1)
                 finish(s - 2, 0, "s")
                 mm2(s - 2, 2)
-            if s + 1 < NCHUNKS:
-                quantize_x(s + 1)
-            if s == 3:
-                prepare_kv(1)
+            if s in COLUMNS:
+                turn_columns(COLUMNS[s])
             if new:
                 add_bias(s, 2)
                 squares(s, 2)
-            if s + 2 < NCHUNKS:
+            for k, j in jobs[3:4]:
+                widen(k, 2, j, "s")
+            if fill and s > 0:
                 interleave(s + 2, 2, 4, "g")
-            if s + 3 < NCHUNKS:
-                widen(s + 3, 2, "s")
             if s + 1 < NCHUNKS:
                 mm1(s + 1, 0)
+            if mid:
+                gating(s - 1, 2)
             if old:
                 finish(s - 2, 1, "v")
                 mm2(s - 2, 3)
-            if mid:
-                gating(s - 1, 2)
             if new:
                 make_gate(s, 0)
             if old:
                 finish(s - 2, 2, "s")
-            if s + 2 < NCHUNKS:
+            if fill and s > 0:
                 interleave(s + 2, 3, 4, "g")
-            if mid and sbuf_gated(s - 1, 3):
-                make_gate_sbuf(s - 1, 3)
             if new:
                 add_bias(s, 3)
                 squares(s, 3)
+                root(s)
+            for k, j in jobs[1:2]:
+                widen(k, 2, j, "s")
             if s + 1 < NCHUNKS:
                 mm1(s + 1, 1)
-            if s + 3 < NCHUNKS:
-                widen(s + 3, 3, "s")
+            if s == 0:
+                for ii in range(4, 10):
+                    mask_pieces(ii, nc.gpsimd)
+                for i in range(2):
+                    interleave(2, i, 4, "g")
+            if s == 1:
+                for i in range(4):
+                    interleave_wo(i)
+            if s in (1, 2, 3, 4):
+                spread_rho(4 * (s - 1))
+            if FIRST_TURNED_GATE <= s < NCHUNKS:
+                gate_columns(s)
             if mid:
                 gating(s - 1, 3)
                 turn(s - 1, 1)
@@ -409,8 +483,10 @@ def tile_hydraattention_pb_t_kernel(tc, x_bytes, x_scale, mask, W_q, b_q, kv_kno
                 make_gate(s, 1)
             if old:
                 finish(s - 2, 3, "v")
+            for ii in MASKS.get(s, ()):
+                mask_pieces(ii, nc.gpsimd)
+            if s == 3:
+                prepare_kv(1, nc.gpsimd)
 
-        for j in range(PACK):
-            widen(2, j, "s")
         for s in range(NCHUNKS + 2):
             step(s)

@@ -30,8 +30,7 @@ Q = 8
 FLOPS = 2 * 2 * B * N * C * C
 
 X_LOADS = ((0, 0, 512), (0, 512, 512), (0, 1024, 1024), (0, 2048, 2048), (1, 0, 2048), (1, 2048, 2048))
-FIRST_TURNED_GATE = 3
-COLUMNS = {2: 0, 5: 1}
+FIRST_SBUF_GATE = 3
 MASKS = {1: range(10, 14), 2: range(14, 16)}
 A1 = "v"
 
@@ -119,6 +118,8 @@ def tile_hydraattention_pb_t_kernel(tc, x_bytes, x_scale, mask, W_q, b_q, kv_kno
             src = planes[k][:, :, part * w : (part + 1) * w].rearrange("p j w -> p w j")
             if eng == "g":
                 nc.gpsimd.tensor_scalar(out=dst, in0=src, scalar1=1.0, scalar2=0.0, op0=ALU.mult, op1=ALU.add)
+            elif eng == "s":
+                nc.scalar.copy(out=dst, in_=src)
             else:
                 nc.vector.tensor_copy(out=dst, in_=src)
 
@@ -249,11 +250,11 @@ def tile_hydraattention_pb_t_kernel(tc, x_bytes, x_scale, mask, W_q, b_q, kv_kno
         widen(2, 2, 0, "s")
         widen(2, 2, 1, "s")
 
-        kv_rows = []
-        kcol = []
-        dcol = []
+        kv_rows = [None, None]
+        kvk = [None, None]
+        dkv = [None, None]
 
-        def prepare_kv(img, eng):
+        def prepare_rows(img, eng):
             parts = []
             for raw, rows, nm in ((kv_raw[img][0], rows_k, "a"), (kv_raw[img][1], rows_m, "b")):
                 r = keep.tile([P, C], BF16, name=f"kv_{nm}{img}")
@@ -262,34 +263,17 @@ def tile_hydraattention_pb_t_kernel(tc, x_bytes, x_scale, mask, W_q, b_q, kv_kno
                 parts.append(r)
             r = keep.tile([P, C], BF16, name=f"kv_rows{img}", align_bytes=64)
             eng.tensor_add(out=r[:], in0=parts[0][:], in1=parts[1][:])
-            kv_rows.append(r)
+            kv_rows[img] = r
 
-        col_ps = {}
-
-        def turn_columns(img):
-            col_ps[img] = psum.tile([P, 4, P], BF16, name="kv_ps", tag="tr")
-            for r in range(4):
-                nc.tensor.transpose(col_ps[img][:, r, :], kv_rows[img][:, r * P : (r + 1) * P], ident_b[:])
-
-        def take_columns(img):
-            k = keep.tile([P, 4], F32, name=f"kcol{img}")
-            d = keep.tile([P, 4], F32, name=f"dcol{img}")
-            ps = col_ps.pop(img)
-            nc.vector.tensor_copy(out=k[:], in_=ps[:, :, 0])
-            nc.vector.tensor_sub(out=d[:], in0=ps[:, :, 3], in1=k[:])
-            kcol.append(k)
-            dcol.append(d)
-
-        n_tg = NCHUNKS - FIRST_TURNED_GATE
-        rho_bc = keep.tile([P, n_tg, TILE], F32, name="rho_bc", align_bytes=64)
-
-        def spread_rho(a):
-            n = min(4, n_tg - a)
-            ps = psum.tile([P, 4, TILE], F32, name="rho_ps", tag="tr")
-            for i in range(n):
-                t = (FIRST_TURNED_GATE + a + i) * NT + NT - 1
-                nc.tensor.transpose(ps[:, i, :], v[:, 1, t : t + 1].to_broadcast([P, P]), ident[:])
-            nc.scalar.copy(out=rho_bc[:, a : a + n, :], in_=ps[:, 0:n, :])
+        def prepare_gate(img):
+            a = keep.tile([P, C], BF16, name=f"kvk{img}")
+            d_raw = keep.tile([P, C], F32, name=f"d_raw{img}")
+            d = keep.tile([P, C], F32, name=f"dkv{img}")
+            g_affine(a[:].rearrange("p (u m e) -> p u m e", u=2, e=2), kv_raw[img][0][:].rearrange("p (m u e) -> p u m e", u=2, e=2), 1.0, 0.0)
+            nc.gpsimd.tensor_sub(out=d_raw[:], in0=kv_raw[img][1][:], in1=kv_raw[img][0][:])
+            g_affine(d[:].rearrange("p (u m e) -> p u m e", u=2, e=2), d_raw[:].rearrange("p (m u e) -> p u m e", u=2, e=2), 1.0, 0.0)
+            kvk[img] = a
+            dkv[img] = d
 
         wo_grouped = keep.tile([P, C, PACK], BF16, name="wo_grouped", align_bytes=64)
         wo_codes = keep.tile([P, C], U32, name="wo_codes", align_bytes=64)
@@ -302,27 +286,17 @@ def tile_hydraattention_pb_t_kernel(tc, x_bytes, x_scale, mask, W_q, b_q, kv_kno
                 scalar1=1.0, scalar2=0.0, op0=ALU.mult, op1=ALU.add,
             )
 
-        def turned(k, i):
-            return i == NT - 1 and k >= FIRST_TURNED_GATE
-
-        gate_t = {}
-
-        def gate_columns(k):
-            img = k // PER_IMG
-            gate_t[k] = work.tile([P, 4, TILE], F32, name="gate_t", align_bytes=64)
-            for r in range(4):
-                nc.gpsimd.tensor_scalar(out=gate_t[k][:, r, :], in0=rho_bc[:, k - FIRST_TURNED_GATE, :], scalar1=dcol[img][:, r : r + 1],
-                                        scalar2=kcol[img][:, r : r + 1], op0=ALU.mult, op1=ALU.add)
+        def in_sbuf(k, i):
+            return i == NT - 1 and k >= FIRST_SBUF_GATE
 
         def make_gate(k, i):
             t = k * NT + i
             img = k // PER_IMG
-            gate[k, i] = psum.tile([P, C], F32, name="gate")
-            if turned(k, i):
-                g = gate_t.pop(k)
-                for r in range(4):
-                    nc.tensor.transpose(gate[k, i][:, r * P : (r + 1) * P], g[:, r, :], ident[:])
+            if in_sbuf(k, i):
+                gate[k, i] = work.tile([P, C], F32, name="gate_sb", bufs=2)
+                nc.vector.scalar_tensor_tensor(out=gate[k, i][:], in0=dkv[img][:], scalar=v[:, 1, t : t + 1], in1=kvk[img][:], op0=ALU.mult, op1=ALU.add)
             else:
+                gate[k, i] = psum.tile([P, C], F32, name="gate")
                 nc.tensor.matmul(gate[k, i][:], lhsT=ptm[:, t % BLK, t // BLK, :], rhs=kv_rows[img][:], start=True, stop=True)
 
         def add_bias(k, i):
@@ -391,15 +365,10 @@ def tile_hydraattention_pb_t_kernel(tc, x_bytes, x_scale, mask, W_q, b_q, kv_kno
             if new:
                 add_bias(s, 0)
                 mm1(s, 2)
-            if s - 1 in COLUMNS:
-                take_columns(COLUMNS[s - 1])
             if s == 0:
                 nc.vector.tensor_copy(out=pt[:], in_=pt_ps[:])
             if old:
                 unload(s - 2, 1)
-            if fill and s > 0:
-                interleave(s + 2, 0, 4, "g")
-                interleave(s + 2, 1, 4, "g")
             if new:
                 squares(s, 0)
             for k, j in jobs[0:1]:
@@ -415,13 +384,14 @@ def tile_hydraattention_pb_t_kernel(tc, x_bytes, x_scale, mask, W_q, b_q, kv_kno
             for k, j in jobs[2:3]:
                 widen(k, 2, j, "s")
             if s == 0:
-                prepare_kv(0, nc.vector)
+                prepare_rows(0, nc.vector)
                 for ii in range(4):
                     mask_pieces(ii, nc.vector)
             if mid:
                 gating(s - 1, 1)
                 turn(s - 1, 0)
-                make_gate(s - 1, 3)
+                if not in_sbuf(s - 1, 3):
+                    make_gate(s - 1, 3)
                 unload(s - 1, 0)
             if s == 1:
                 interleave(2, 1, 2, "v")
@@ -432,19 +402,20 @@ def tile_hydraattention_pb_t_kernel(tc, x_bytes, x_scale, mask, W_q, b_q, kv_kno
             if old:
                 mm2(s - 2, 0)
                 mm2(s - 2, 1)
-                finish(s - 2, 0, "s")
-                mm2(s - 2, 2)
-            if s in COLUMNS:
-                turn_columns(COLUMNS[s])
+            if mid and in_sbuf(s - 1, 3):
+                make_gate(s - 1, 3)
             if new:
                 add_bias(s, 2)
                 squares(s, 2)
+            if fill and s > 0:
+                interleave(s + 2, 0, 2, "s")
             for k, j in jobs[3:4]:
                 widen(k, 2, j, "s")
-            if fill and s > 0:
-                interleave(s + 2, 2, 4, "g")
             if s + 1 < NCHUNKS:
                 mm1(s + 1, 0)
+            if old:
+                finish(s - 2, 0, "v")
+                mm2(s - 2, 2)
             if mid:
                 gating(s - 1, 2)
             if old:
@@ -452,10 +423,6 @@ def tile_hydraattention_pb_t_kernel(tc, x_bytes, x_scale, mask, W_q, b_q, kv_kno
                 mm2(s - 2, 3)
             if new:
                 make_gate(s, 0)
-            if old:
-                finish(s - 2, 2, "s")
-            if fill and s > 0:
-                interleave(s + 2, 3, 4, "g")
             if new:
                 add_bias(s, 3)
                 squares(s, 3)
@@ -472,10 +439,10 @@ def tile_hydraattention_pb_t_kernel(tc, x_bytes, x_scale, mask, W_q, b_q, kv_kno
             if s == 1:
                 for i in range(4):
                     interleave_wo(i)
-            if s in (1, 2, 3, 4):
-                spread_rho(4 * (s - 1))
-            if FIRST_TURNED_GATE <= s < NCHUNKS:
-                gate_columns(s)
+            if fill and s > 0:
+                interleave(s + 2, 1, 2, "s")
+            if old:
+                finish(s - 2, 2, "v")
             if mid:
                 gating(s - 1, 3)
                 turn(s - 1, 1)
@@ -485,8 +452,11 @@ def tile_hydraattention_pb_t_kernel(tc, x_bytes, x_scale, mask, W_q, b_q, kv_kno
                 finish(s - 2, 3, "v")
             for ii in MASKS.get(s, ()):
                 mask_pieces(ii, nc.gpsimd)
+            if s == 1:
+                prepare_gate(0)
             if s == 3:
-                prepare_kv(1, nc.gpsimd)
+                prepare_rows(1, nc.gpsimd)
+                prepare_gate(1)
 
         for s in range(NCHUNKS + 2):
             step(s)

@@ -30,9 +30,9 @@ Q = 8
 FLOPS = 2 * 2 * B * N * C * C
 
 X_LOADS = ((0, 0, 512), (0, 512, 512), (0, 1024, 1024), (0, 2048, 2048), (1, 0, 2048), (1, 2048, 2048))
-FIRST_SBUF_GATE = 3
-MASKS = {1: range(10, 14), 2: range(14, 16)}
-A1 = "v"
+V_WIDENS = (9, 11)
+LIGHT = (2, 3, 4, 5, 6, 7, 17)
+TURNED_GATES = [(k, i) for k in range(2) for i in range(4)] + [(k, 3) for k in range(3, 8)]
 
 
 def tile_hydraattention_pb_t_kernel(tc, x_bytes, x_scale, mask, W_q, b_q, kv_know, kv_mask, W_out, b_out, out):
@@ -59,21 +59,22 @@ def tile_hydraattention_pb_t_kernel(tc, x_bytes, x_scale, mask, W_q, b_q, kv_kno
             x_tiles.append((img * N + t0, width, t))
 
         load_x(0)
-        wq_raw = keep.tile([P, PACK, C], BF16, name="wq_raw")
-        nc.sync.dma_start(out=wq_raw[:], in_=W_q.rearrange("(p j) w -> p j w", j=PACK))
-        bq_raw = keep.tile([P, C], BF16, name="bq_raw")
-        nc.sync.dma_start(out=bq_raw[:], in_=b_q.partition_broadcast(P))
-        load_x(1)
         kv_raw = []
 
         def load_kv(img):
-            a = keep.tile([P, C], BF16, name=f"kvk_raw{img}")
-            nc.sync.dma_start(out=a[:], in_=kv_know[img].rearrange("o c -> (o c)").partition_broadcast(P))
-            b = keep.tile([P, C], BF16, name=f"kvm_raw{img}")
-            nc.sync.dma_start(out=b[:], in_=kv_mask[img].rearrange("o c -> (o c)").partition_broadcast(P))
-            kv_raw.append((a, b))
+            t = keep.tile([P, C], BF16, name=f"kv_raw{img}")
+            nc.vector.memset(t[96:P, :], 0.0)
+            nc.sync.dma_start(out=t[0:48, :], in_=kv_know[img].rearrange("o c -> (o c)").partition_broadcast(48))
+            nc.sync.dma_start(out=t[48:96, :], in_=kv_mask[img].rearrange("o c -> (o c)").partition_broadcast(48))
+            kv_raw.append(t)
 
+        wq_raw = keep.tile([P, PACK, C], BF16, name="wq_raw")
+        nc.sync.dma_start(out=wq_raw[:], in_=W_q.rearrange("(p j) w -> p j w", j=PACK))
         load_kv(0)
+        bq_raw = keep.tile([P, C], BF16, name="bq_raw")
+        nc.sync.dma_start(out=bq_raw[:], in_=b_q.partition_broadcast(P))
+        load_x(1)
+
         load_x(2)
         wo_raw = keep.tile([P, PACK, C], BF16, name="wo_raw")
         nc.sync.dma_start(out=wo_raw[:], in_=W_out.rearrange("(p j) w -> p j w", j=PACK))
@@ -108,7 +109,8 @@ def tile_hydraattention_pb_t_kernel(tc, x_bytes, x_scale, mask, W_q, b_q, kv_kno
 
         def batch_half(s, half):
             if s not in batch:
-                batch[s] = work.tile([P, 2, CHUNK, PACK], BF16, name="batch", align_bytes=64)
+                nm = "batch" if s >= 2 else f"batch{s + 1}"
+                batch[s] = work.tile([P, 2, CHUNK, PACK], BF16, name=nm, bufs=1, align_bytes=64)
             return batch[s][:, half]
 
         def interleave(k, part, parts, eng):
@@ -122,6 +124,15 @@ def tile_hydraattention_pb_t_kernel(tc, x_bytes, x_scale, mask, W_q, b_q, kv_kno
                 nc.scalar.copy(out=dst, in_=src)
             else:
                 nc.vector.tensor_copy(out=dst, in_=src)
+
+        def quantize_half(s, h):
+            if h == 0:
+                codes = work.tile([P, 2, CHUNK], U32, name="codes", align_bytes=64)
+                scales = work.tile([P, 2, CHUNK], U8, name="scales", align_bytes=64)
+                gcodes[s - 2] = (codes[:, 1], scales[:, 1])
+            codes, scales = gcodes[s - 2]
+            cols = slice(h * 256, (h + 1) * 256)
+            nc.vector.quantize_mx(out=codes[:, cols].bitcast(FP8X4), scales=scales[:, cols], in_=batch[s][:, 1, cols].rearrange("p w j -> p (w j)"))
 
         def quantize(s):
             lo = 0 if s + 1 < NCHUNKS else 1
@@ -140,19 +151,14 @@ def tile_hydraattention_pb_t_kernel(tc, x_bytes, x_scale, mask, W_q, b_q, kv_kno
 
         warm = keep.tile([P, 1], F32, name="warm")
         nc.vector.memset(warm[:], 1.0)
-        nc.scalar.activation(out=warm[:], in_=warm[:], func=ACT.Sqrt)
+        nc.scalar.activation(out=warm[:], in_=warm[:], func=ACT.Abs_reciprocal_sqrt)
         ident = keep.tile([P, P], F32, name="ident", align_bytes=64)
         make_identity(nc, ident[:])
         ident_b = keep.tile([P, P], BF16, name="ident_b", align_bytes=64)
         nc.vector.tensor_copy(out=ident_b[:], in_=ident[:])
-        by_tile = ident[:].rearrange("p (i q) -> p i q", q=Q)
         sel = keep.tile([P, BLK], F32, name="sel")
-        nc.vector.tensor_reduce(out=sel[:], in_=by_tile, axis=AXIS.X, op=ALU.add)
-        rows_k = keep.tile([P, 1], F32, name="rows_k")
-        nc.vector.tensor_reduce(out=rows_k[:], in_=by_tile[:, :, 0:3], axis=AXIS.XY, op=ALU.add)
-        rows_m = keep.tile([P, 1], F32, name="rows_m")
-        nc.vector.tensor_reduce(out=rows_m[:], in_=by_tile[:, :, 3:6], axis=AXIS.XY, op=ALU.add)
-        pieces = keep.tile([P, NTILES, Q], BF16, name="pieces", align_bytes=64)
+        nc.vector.tensor_reduce(out=sel[:], in_=ident[:].rearrange("p (q i) -> p i q", q=Q), axis=AXIS.X, op=ALU.add)
+        pieces = keep.tile([P, NTILES // BLK, Q, BLK], BF16, name="pieces", align_bytes=64)
         nc.vector.memset(pieces[:], 0.0)
 
         mrow32 = keep.tile([P, P], F32, name="mrow32", align_bytes=64)
@@ -168,24 +174,23 @@ def tile_hydraattention_pb_t_kernel(tc, x_bytes, x_scale, mask, W_q, b_q, kv_kno
         sg = keep.tile([P, NTILES], F32, name="sg")
         inv_sg = keep.tile([P, NTILES], F32, name="inv_sg")
         v = keep.tile([P, 2, NTILES], F32, name="v")
-        pv = pieces[:, :, 0:6].rearrange("p i (v q) -> p v i q", q=3)
         rest = [keep.tile([P, 2, NTILES], F32, name=f"rest{i}") for i in range(2)]
 
         def g_affine(dst, src, a, b):
             nc.gpsimd.tensor_scalar(out=dst, in0=src, scalar1=a, scalar2=b, op0=ALU.mult, op1=ALU.add)
 
-        g_affine(t1[:], m[:], 1.4, -1.7)
-        g_affine(t3[:], m[:], 0.7, 0.0)
-        nc.gpsimd.tensor_mul(out=t2[:], in0=t1[:], in1=m[:])
-        nc.gpsimd.tensor_mul(out=t4[:], in0=t3[:], in1=m[:])
-        g_affine(sg[:], t2[:], 1.0, 1.0)
-
         widen(0, 1, 0, "s")
         widen(0, 1, 1, "v")
         widen(0, 1, 2, "v")
+        nc.vector.tensor_scalar(out=t1[:], in0=m[:], scalar1=1.4, scalar2=-1.7, op0=ALU.mult, op1=ALU.add)
+        nc.vector.tensor_scalar(out=t3[:], in0=m[:], scalar1=0.7, scalar2=None, op0=ALU.mult)
         widen(0, 1, 3, "v")
+        nc.vector.tensor_mul(out=t2[:], in0=t1[:], in1=m[:])
+        nc.vector.tensor_mul(out=t4[:], in0=t3[:], in1=m[:])
+        interleave(0, 0, 2, "v")
+        nc.vector.tensor_scalar(out=sg[:], in0=t2[:], scalar1=1.0, scalar2=None, op0=ALU.add)
+        interleave(0, 1, 2, "v")
         nc.vector.reciprocal(out=inv_sg[:], in_=sg[:])
-        interleave(0, 0, 1, "v")
 
         wq_grouped = keep.tile([P, C, PACK], BF16, name="wq_grouped", align_bytes=64)
         wq_codes = keep.tile([P, C], U32, name="wq_codes", align_bytes=64)
@@ -199,20 +204,25 @@ def tile_hydraattention_pb_t_kernel(tc, x_bytes, x_scale, mask, W_q, b_q, kv_kno
             else:
                 nc.scalar.copy(out=dst, in_=src)
 
+        permute_wq(0, "s")
         permute_wq(1, "s")
-        permute_wq(0, "g")
         nc.gpsimd.tensor_mul(out=v[:, 1, :], in0=t4[:], in1=inv_sg[:])
         quantize(-1)
-        nc.vector.quantize_mx(out=wq_codes[:].bitcast(FP8X4), scales=wq_scales[:], in_=wq_grouped[:].rearrange("p w j -> p (w j)"))
         bq = keep.tile([P, C], BF16, name="bq")
         nc.scalar.copy(out=bq[:].rearrange("p (u m e) -> p u m e", u=2, e=2), in_=bq_raw[:].rearrange("p (m u e) -> p u m e", u=2, e=2))
 
-        g_affine(v[:, 0, :], v[:, 1, :], -1.0, 1.0)
-        g_affine(pv[:, :, :, 0], v[:], 1.0, 0.0)
-        nc.gpsimd.tensor_sub(out=rest[0][:], in0=v[:], in1=pv[:, :, :, 0])
-        g_affine(pv[:, :, :, 1], rest[0][:], 1.0, 0.0)
-        nc.gpsimd.tensor_sub(out=rest[1][:], in0=rest[0][:], in1=pv[:, :, :, 1])
-        g_affine(pv[:, :, :, 2], rest[1][:], 1.0, 0.0)
+
+        def piece(i):
+            res = v if i == 0 else rest[i - 1]
+            for h in range(2):
+                src = res[:, h, :].rearrange("p (b i) -> p b i", i=BLK)
+                g_affine(pieces[:, :, 3 * h + i, :], src, 1.0, 0.0)
+                if i < 2:
+                    nc.gpsimd.tensor_sub(out=rest[i][:, h, :].rearrange("p (b i) -> p b i", i=BLK), in0=src, in1=pieces[:, :, 3 * h + i, :])
+
+        nc.vector.quantize_mx(out=wq_codes[:].bitcast(FP8X4), scales=wq_scales[:], in_=wq_grouped[:].rearrange("p w j -> p (w j)"))
+        for j in range(PACK):
+            widen(1, 1, j, "v")
 
         q0 = {}
         gate = {}
@@ -235,68 +245,64 @@ def tile_hydraattention_pb_t_kernel(tc, x_bytes, x_scale, mask, W_q, b_q, kv_kno
 
         pt = keep.tile([P, 4, P], BF16, name="pt", align_bytes=64)
         ptm = keep.tile([P, BLK, 4, P], BF16, name="ptm", align_bytes=64)
-        pt_ps = psum.tile([P, 4, P], BF16, name="pt_ps", tag="tr")
-        for b in range(4):
-            nc.tensor.transpose(pt_ps[:, b, :], pieces[:, b * BLK : (b + 1) * BLK, :].rearrange("p i q -> p (i q)"), ident_b[:])
 
-        def mask_pieces(ii, eng):
-            eng.tensor_scalar(out=ptm[:, ii], in0=pt[:], scalar1=sel[:, ii : ii + 1], scalar2=1.0, op0=ALU.mult, op1=ALU.mult)
+        def turn_pieces():
+            ps = psum.tile([P, 4, P], BF16, name="pt_ps", tag="tr")
+            for b in range(4):
+                nc.tensor.transpose(ps[:, b, :], pieces[:, b].rearrange("p q i -> p (q i)"), ident_b[:])
+            nc.scalar.copy(out=pt[:], in_=ps[:])
 
-        for j in range(PACK):
-            widen(1, 1, j, A1)
-        for i in range(4):
-            interleave(1, i, 4, "g")
+        def mask_pieces(ii):
+            nc.vector.tensor_scalar(out=ptm[:, ii], in0=pt[:], scalar1=sel[:, ii : ii + 1], scalar2=None, op0=ALU.mult)
 
-        widen(2, 2, 0, "s")
-        widen(2, 2, 1, "s")
+        interleave(1, 0, 2, "g")
+        interleave(1, 1, 2, "g")
 
-        kv_rows = [None, None]
-        kvk = [None, None]
-        dkv = [None, None]
+        kv_rows = []
 
-        def prepare_rows(img, eng):
-            parts = []
-            for raw, rows, nm in ((kv_raw[img][0], rows_k, "a"), (kv_raw[img][1], rows_m, "b")):
-                r = keep.tile([P, C], BF16, name=f"kv_{nm}{img}")
-                eng.tensor_scalar(out=r[:].rearrange("p (u m e) -> p u m e", u=2, e=2), in0=raw[:].rearrange("p (m u e) -> p u m e", u=2, e=2),
-                                  scalar1=rows[:], scalar2=1.0, op0=ALU.mult, op1=ALU.mult)
-                parts.append(r)
+        def permute_rows(img):
             r = keep.tile([P, C], BF16, name=f"kv_rows{img}", align_bytes=64)
-            eng.tensor_add(out=r[:], in0=parts[0][:], in1=parts[1][:])
-            kv_rows[img] = r
+            nc.scalar.copy(out=r[:].rearrange("p (u m e) -> p u m e", u=2, e=2), in_=kv_raw[img][:].rearrange("p (m u e) -> p u m e", u=2, e=2))
+            kv_rows.append(r)
 
-        def prepare_gate(img):
-            a = keep.tile([P, C], BF16, name=f"kvk{img}")
-            d_raw = keep.tile([P, C], F32, name=f"d_raw{img}")
-            d = keep.tile([P, C], F32, name=f"dkv{img}")
-            g_affine(a[:].rearrange("p (u m e) -> p u m e", u=2, e=2), kv_raw[img][0][:].rearrange("p (m u e) -> p u m e", u=2, e=2), 1.0, 0.0)
-            nc.gpsimd.tensor_sub(out=d_raw[:], in0=kv_raw[img][1][:], in1=kv_raw[img][0][:])
-            g_affine(d[:].rearrange("p (u m e) -> p u m e", u=2, e=2), d_raw[:].rearrange("p (m u e) -> p u m e", u=2, e=2), 1.0, 0.0)
-            kvk[img] = a
-            dkv[img] = d
+        kcol = keep.tile([P, 4], F32, name="kcol")
+        dcol = keep.tile([P, 4], F32, name="dcol")
+
+        def take_columns():
+            ps = psum.tile([P, 4, P], BF16, name="kv_ps", tag="tr")
+            for r in range(4):
+                nc.tensor.transpose(ps[:, r, :], kv_rows[0][:, r * P : (r + 1) * P], ident_b[:])
+            nc.vector.tensor_copy(out=kcol[:], in_=ps[:, :, 0])
+            nc.vector.tensor_sub(out=dcol[:], in0=ps[:, :, 48], in1=kcol[:])
+
+        gate_t = {}
+
+        def spread_rho(todo):
+            ps = psum.tile([P, 4, TILE], F32, name="rho_ps", tag="tr")
+            for n, (k, i) in enumerate(todo):
+                t = k * NT + i
+                nc.tensor.transpose(ps[:, n, :], v[:, 1, t : t + 1].to_broadcast([P, P]), ident[:])
+            return ps
+
+        def gate_columns(todo, ps, first=0):
+            for n, (k, i) in enumerate(todo, first):
+                gate_t[k, i] = keep.tile([P, 4, TILE], F32, name=f"gate_t{k}_{i}", align_bytes=64)
+                for r in range(4):
+                    nc.scalar.activation(out=gate_t[k, i][:, r, :], in_=ps[:, n, :], func=ACT.Identity, scale=dcol[:, r : r + 1], bias=kcol[:, r : r + 1])
 
         wo_grouped = keep.tile([P, C, PACK], BF16, name="wo_grouped", align_bytes=64)
         wo_codes = keep.tile([P, C], U32, name="wo_codes", align_bytes=64)
         wo_scales = keep.tile([P, C], U8, name="wo_scales", align_bytes=64)
 
-        def interleave_wo(i):
-            nc.gpsimd.tensor_scalar(
-                out=wo_grouped[:, i * 128 : (i + 1) * 128, :],
-                in0=wo_raw[:, :, i * 128 : (i + 1) * 128].rearrange("p j w -> p w j"),
-                scalar1=1.0, scalar2=0.0, op0=ALU.mult, op1=ALU.add,
-            )
-
-        def in_sbuf(k, i):
-            return i == NT - 1 and k >= FIRST_SBUF_GATE
 
         def make_gate(k, i):
             t = k * NT + i
             img = k // PER_IMG
-            if in_sbuf(k, i):
-                gate[k, i] = work.tile([P, C], F32, name="gate_sb", bufs=2)
-                nc.vector.scalar_tensor_tensor(out=gate[k, i][:], in0=dkv[img][:], scalar=v[:, 1, t : t + 1], in1=kvk[img][:], op0=ALU.mult, op1=ALU.add)
+            gate[k, i] = psum.tile([P, C], F32, name="gate")
+            if (k, i) in TURNED_GATES:
+                for r in range(4):
+                    nc.tensor.transpose(gate[k, i][:, r * P : (r + 1) * P], gate_t[k, i][:, r, :], ident[:])
             else:
-                gate[k, i] = psum.tile([P, C], F32, name="gate")
                 nc.tensor.matmul(gate[k, i][:], lhsT=ptm[:, t % BLK, t // BLK, :], rhs=kv_rows[img][:], start=True, stop=True)
 
         def add_bias(k, i):
@@ -304,18 +310,15 @@ def tile_hydraattention_pb_t_kernel(tc, x_bytes, x_scale, mask, W_q, b_q, kv_kno
             nc.vector.tensor_add(out=qb[k, i][:], in0=q0.pop((k, i))[:], in1=bq[:])
 
         def squares(k, i):
-            if i == 0:
+            if k not in ss:
                 ss[k] = work.tile([P, NT], F32, name="ss")
             t = k * NT + i
-            junk = work.tile([P, C], BF16, name="junk", bufs=2)
+            junk = work.tile([P, C], BF16, name="junk", bufs=8)
             nc.scalar.activation(out=junk[:], in_=qb[k, i][:], func=ACT.Square, scale=inv_sg[:, t : t + 1], accum_out=ss[k][:, i : i + 1])
 
         def root(k):
-            nc.scalar.activation(out=ss[k][:], in_=ss[k][:], func=ACT.Sqrt)
-
-        def recip(k):
             rn[k] = work.tile([P, NT], F32, name="rn")
-            nc.vector.reciprocal(out=rn[k][:], in_=ss[k][:])
+            nc.scalar.activation(out=rn[k][:], in_=ss[k][:], func=ACT.Abs_reciprocal_sqrt)
 
         def gating(k, i):
             gt[k, i] = work.tile([P, C], BF16, name="gt", bufs=6, align_bytes=64)
@@ -339,124 +342,186 @@ def tile_hydraattention_pb_t_kernel(tc, x_bytes, x_scale, mask, W_q, b_q, kv_kno
             nc.tensor.matmul_mx(out=y_ps[k, i][:], lhsT=codes[:, cols].bitcast(FP8X4), lhsT_scale=scales[:, cols],
                                 rhs=wo_codes[:].bitcast(FP8X4), rhs_scale=wo_scales[:], start=True, stop=True)
 
+        y_sb = {}
+
         def finish(k, i, eng):
-            y = work.tile([P, C], F32, name="y", bufs=8)
+            h = i // 2
+            if (k, h) not in y_sb:
+                y_sb[k, h] = work.tile([P, 2, C], F32, name=f"y{h}", bufs=3)
+            y = y_sb[k, h][:, i % 2, :]
             src = y_ps.pop((k, i))
             if eng == "v":
-                nc.vector.tensor_add(out=y[:], in0=src[:], in1=bo[:])
+                nc.vector.tensor_add(out=y, in0=src[:], in1=bo[:])
             else:
-                nc.scalar.copy(out=y[:], in_=src[:])
-                nc.gpsimd.tensor_add(out=y[:], in0=y[:], in1=bo[:])
-            t = k * NT + i
-            nc.sync.dma_start(out=out_rows[t * TILE : (t + 1) * TILE, :], in_=y[:])
+                nc.scalar.copy(out=y, in_=src[:])
 
-        def widen_jobs(s):
-            if s < 2:
-                return [(2, 2), (2, 3), (4, 0)] if s == 0 else [(4, 1), (4, 2), (4, 3)]
-            pair = s + 4 - s % 2
-            return [(pair, 2 * (s % 2) + i) for i in range(2)] if pair < NCHUNKS else []
+        def add_out(k, i):
+            y = y_sb[k, i // 2][:, i % 2, :]
+            nc.gpsimd.tensor_add(out=y, in0=y, in1=bo[:])
+
+        def store(k, h):
+            t0 = (k * NT + 2 * h) * TILE
+            nc.sync.dma_start(out=out_rows[t0 : t0 + 2 * TILE, :].rearrange("(a p) c -> p a c", p=P), in_=y_sb.pop((k, h))[:])
+
+        def store_one(k, i):
+            t0 = (k * NT + i) * TILE
+            nc.sync.dma_start(out=out_rows[t0 : t0 + TILE, :], in_=y_sb[k, i // 2][:, i % 2, :])
 
         def step(s):
             new = s < NCHUNKS
             mid = 0 <= s - 1 < NCHUNKS
             old = 0 <= s - 2 < NCHUNKS
-            jobs = widen_jobs(s)
             fill = s + 2 < NCHUNKS
-            if new:
-                add_bias(s, 0)
-                mm1(s, 2)
-            if s == 0:
-                nc.vector.tensor_copy(out=pt[:], in_=pt_ps[:])
-            if old:
-                unload(s - 2, 1)
-            if new:
-                squares(s, 0)
-            for k, j in jobs[0:1]:
-                widen(k, 2, j, "s")
-            if mid:
-                recip(s - 1)
-                gating(s - 1, 0)
-                make_gate(s - 1, 2)
-            if new:
-                add_bias(s, 1)
-                squares(s, 1)
-                mm1(s, 3)
-            for k, j in jobs[2:3]:
-                widen(k, 2, j, "s")
-            if s == 0:
-                prepare_rows(0, nc.vector)
-                for ii in range(4):
-                    mask_pieces(ii, nc.vector)
-            if mid:
-                gating(s - 1, 1)
-                turn(s - 1, 0)
-                if not in_sbuf(s - 1, 3):
-                    make_gate(s - 1, 3)
-                unload(s - 1, 0)
-            if s == 1:
-                interleave(2, 1, 2, "v")
+            pair = s + 4 - s % 2
+            todo = [g for g in TURNED_GATES if g[0] == s]
+            if s in V_WIDENS:
+                widen(pair, 2, 3, "v")
+            if s >= 2:
+                quantize(s)
             if s == 2:
                 nc.vector.quantize_mx(out=wo_codes[:].bitcast(FP8X4), scales=wo_scales[:], in_=wo_grouped[:].rearrange("p w j -> p (w j)"))
-            if s + 1 < NCHUNKS or old:
-                quantize(s)
+            if s >= 2 and pair < NCHUNKS:
+                widen(pair, 2, 2 * (s % 2), "s")
+                if s not in V_WIDENS:
+                    widen(pair, 2, 2 * (s % 2) + 1, "s")
+            if fill and s >= 2:
+                interleave(s + 2, 0, 2, "g")
+                interleave(s + 2, 1, 2, "g")
             if old:
                 mm2(s - 2, 0)
                 mm2(s - 2, 1)
-            if mid and in_sbuf(s - 1, 3):
-                make_gate(s - 1, 3)
-            if new:
-                add_bias(s, 2)
-                squares(s, 2)
-            if fill and s > 0:
-                interleave(s + 2, 0, 2, "s")
-            for k, j in jobs[3:4]:
-                widen(k, 2, j, "s")
-            if s + 1 < NCHUNKS:
-                mm1(s + 1, 0)
-            if old:
-                finish(s - 2, 0, "v")
-                mm2(s - 2, 2)
-            if mid:
-                gating(s - 1, 2)
-            if old:
-                finish(s - 2, 1, "v")
-                mm2(s - 2, 3)
-            if new:
-                make_gate(s, 0)
-            if new:
-                add_bias(s, 3)
-                squares(s, 3)
-                root(s)
-            for k, j in jobs[1:2]:
-                widen(k, 2, j, "s")
-            if s + 1 < NCHUNKS:
-                mm1(s + 1, 1)
+            if s <= 1:
+                add_bias(s, 0)
+                add_bias(s, 1)
             if s == 0:
-                for ii in range(4, 10):
-                    mask_pieces(ii, nc.gpsimd)
-                for i in range(2):
-                    interleave(2, i, 4, "g")
-            if s == 1:
-                for i in range(4):
-                    interleave_wo(i)
-            if fill and s > 0:
-                interleave(s + 2, 1, 2, "s")
+                take_columns()
+                rho0 = spread_rho(todo)
+                gate_columns(todo[:2], rho0)
+            if mid:
+                gating(s - 1, 1)
+                gating(s - 1, 0)
+                make_gate(s - 1, 2)
+                make_gate(s - 1, 3)
+                turn(s - 1, 0)
+            by_scalar = (1,) if s in LIGHT else (1, 0)
             if old:
-                finish(s - 2, 2, "v")
+                for i in by_scalar:
+                    finish(s - 2, i, "s")
+                    add_out(s - 2, i)
+            if mid and s >= 2:
+                unload(s - 1, 0)
+            if new and s >= 2:
+                add_bias(s, 0)
+                add_bias(s, 1)
+            if new:
+                mm1(s, 2)
+                mm1(s, 3)
+                squares(s, 1)
+                squares(s, 0)
+            if s == 1:
+                unload(0, 0)
+            if s == 2:
+                turn_pieces()
+            if old and 0 not in by_scalar:
+                finish(s - 2, 0, "v")
+            if old:
+                mm2(s - 2, 2)
+                mm2(s - 2, 3)
             if mid:
                 gating(s - 1, 3)
+                gating(s - 1, 2)
                 turn(s - 1, 1)
+                unload(s - 1, 1)
             if new:
+                add_bias(s, 3)
+                add_bias(s, 2)
+                squares(s, 3)
+                squares(s, 2)
+                root(s)
+            if s <= 1:
+                for j in range(2):
+                    widen(2 * s + 2, 2, 2 + j, "v")
+                quantize(s)
+            if s == 0:
+                for i in range(4):
+                    interleave(2 + i // 2, i % 2, 2, "g")
+                g_affine(v[:, 0, :], v[:, 1, :], -1.0, 1.0)
+                for i in range(3):
+                    piece(i)
+            if s == 2:
+                for ii in range(8, 12):
+                    mask_pieces(ii)
+            if s + 1 < NCHUNKS:
+                mm1(s + 1, 0)
+                mm1(s + 1, 1)
+            if todo:
+                if s == 0:
+                    gate_columns(todo[2:], rho0, 2)
+                else:
+                    gate_columns(todo, spread_rho(todo))
+            if new:
+                make_gate(s, 0)
                 make_gate(s, 1)
+            if s == 0:
+                widen(4, 2, 0, "s")
+                widen(4, 2, 1, "s")
             if old:
-                finish(s - 2, 3, "v")
-            for ii in MASKS.get(s, ()):
-                mask_pieces(ii, nc.gpsimd)
+                for i in (3, 2):
+                    finish(s - 2, i, "v")
+                store(s - 2, 0)
+                store(s - 2, 1)
+            if s in (2, 3, 4):
+                for ii in [(12, 13, 14, 15), (0, 1, 2, 3), (4, 5, 6, 7)][s - 2]:
+                    mask_pieces(ii)
             if s == 1:
-                prepare_gate(0)
-            if s == 3:
-                prepare_rows(1, nc.gpsimd)
-                prepare_gate(1)
+                nc.vector.tensor_copy(out=wo_grouped[:], in_=wo_raw[:].rearrange("p j w -> p w j"))
+            if s == 5:
+                permute_rows(1)
 
-        for s in range(NCHUNKS + 2):
+        def last_steps():
+            k = NCHUNKS - 1
+            s = NCHUNKS
+            quantize(s)
+            mm2(k - 1, 0)
+            mm2(k - 1, 1)
+            gating(k, 1)
+            gating(k, 0)
+            make_gate(k, 2)
+            make_gate(k, 3)
+            turn(k, 0)
+            finish(k - 1, 1, "s")
+            add_out(k - 1, 1)
+            unload(k, 0)
+            finish(k - 1, 0, "v")
+            store(k - 1, 0)
+            mm2(k - 1, 2)
+            mm2(k - 1, 3)
+            gating(k, 3)
+            gating(k, 2)
+            turn(k, 1)
+            unload(k, 1)
+            quantize_half(s + 1, 0)
+            mm2(k, 0)
+            mm2(k, 1)
+            finish(k - 1, 3, "v")
+            finish(k - 1, 2, "v")
+            store(k - 1, 1)
+            quantize_half(s + 1, 1)
+            finish(k, 0, "s")
+            add_out(k, 0)
+            finish(k, 1, "v")
+            mm2(k, 2)
+            mm2(k, 3)
+            store_one(k, 1)
+            finish(k, 2, "v")
+            store_one(k, 0)
+            finish(k, 3, "v")
+            store_one(k, 2)
+            store_one(k, 3)
+
+        permute_rows(0)
+        widen(2, 2, 0, "s")
+        widen(2, 2, 1, "s")
+        for s in range(NCHUNKS):
             step(s)
+        last_steps()

from contextlib import ExitStack

import concourse.mybir as mybir
from concourse.masks import make_identity

F32 = mybir.dt.float32
BF16 = mybir.dt.bfloat16
U32 = mybir.dt.uint32
U8 = mybir.dt.uint8
FP8 = mybir.dt.float8_e4m3fn
FP8X4 = mybir.dt.float8_e4m3fn_x4
ALU = mybir.AluOpType
ACT = mybir.ActivationFunctionType
AXIS = mybir.AxisListType

B = 2
C = 512
N = 4096
P = 128
PACK = 4
TILE = 128
CHUNK = 512
NT = CHUNK // TILE
NTILES = B * N // TILE
NCHUNKS = B * N // CHUNK
PER_IMG = N // CHUNK
BLK = 16
Q = 8

FLOPS = 2 * 2 * B * N * C * C

X_LOADS = ((0, 0, 512), (0, 512, 512), (0, 1024, 1024), (0, 2048, 2048), (1, 0, 2048), (1, 2048, 2048))
V_WIDENS = (9, 11)
LIGHT = (2, 3, 4, 5, 6, 7, 17)
TURNED_GATES = [(k, i) for k in range(2) for i in range(4)] + [(k, 3) for k in range(3, 8)]


def tile_hydraattention_pb_t_kernel(tc, x_bytes, x_scale, mask, W_q, b_q, kv_know, kv_mask, W_out, b_out, out):
    nc = tc.nc
    out_rows = out.rearrange("b t c -> (b t) c")

    with ExitStack() as ctx:
        keep = ctx.enter_context(tc.tile_pool(name="keep", bufs=1))
        work = ctx.enter_context(tc.tile_pool(name="work", bufs=3))
        psum = ctx.enter_context(tc.psum_pool(name="psum", bufs=2))
        ctx.enter_context(tc.manual_schedule())

        mrow = keep.tile([P, P], BF16, name="mrow")
        nc.vector.memset(mrow[:], 0.0)
        nc.sync.dma_start(out=mrow[0:NTILES, :], in_=mask.rearrange("b o (r q) w -> (b o r) (q w)", q=2))
        xs = keep.tile([P, PACK], F32, name="xs")
        nc.sync.dma_start(out=xs[:], in_=x_scale.rearrange("o (p j) a b -> p (o j a b)", j=PACK))
        x_tiles = []

        def load_x(i):
            img, t0, width = X_LOADS[i]
            t = keep.tile([P, PACK, width], U8, name=f"xb{i}", align_bytes=64)
            nc.sync.dma_start(out=t[:], in_=x_bytes[img].rearrange("(p j) h w -> p j (h w)", j=PACK)[:, :, t0 : t0 + width])
            x_tiles.append((img * N + t0, width, t))

        load_x(0)
        kv_raw = []

        def load_kv(img):
            t = keep.tile([P, C], BF16, name=f"kv_raw{img}")
            nc.vector.memset(t[96:P, :], 0.0)
            nc.sync.dma_start(out=t[0:48, :], in_=kv_know[img].rearrange("o c -> (o c)").partition_broadcast(48))
            nc.sync.dma_start(out=t[48:96, :], in_=kv_mask[img].rearrange("o c -> (o c)").partition_broadcast(48))
            kv_raw.append(t)

        wq_raw = keep.tile([P, PACK, C], BF16, name="wq_raw")
        nc.sync.dma_start(out=wq_raw[:], in_=W_q.rearrange("(p j) w -> p j w", j=PACK))
        load_kv(0)
        bq_raw = keep.tile([P, C], BF16, name="bq_raw")
        nc.sync.dma_start(out=bq_raw[:], in_=b_q.partition_broadcast(P))
        load_x(1)

        load_x(2)
        wo_raw = keep.tile([P, PACK, C], BF16, name="wo_raw")
        nc.sync.dma_start(out=wo_raw[:], in_=W_out.rearrange("(p j) w -> p j w", j=PACK))
        bo = keep.tile([P, C], BF16, name="bo")
        nc.sync.dma_start(out=bo[:], in_=b_out.partition_broadcast(P))
        load_kv(1)
        load_x(3)
        load_x(4)
        load_x(5)

        planes = {}
        xcodes = {}
        gcodes = {}
        batch = {}

        def widen(k, chunks, j, eng):
            t0 = k * CHUNK
            w = chunks * CHUNK
            if j == 0:
                pl = work.tile([P, PACK, 2 * CHUNK], BF16, name="planes", align_bytes=64)
                for c in range(chunks):
                    planes[k + c] = pl[:, :, c * CHUNK : (c + 1) * CHUNK]
                planes["w", k] = pl
            for start, width, t in x_tiles:
                if start <= t0 < start + width:
                    src = t[:, j, t0 - start : t0 - start + w].bitcast(FP8)
            dst = planes["w", k][:, j, 0:w]
            if eng == "s":
                nc.scalar.activation(out=dst, in_=src, func=ACT.Copy, scale=xs[:, j : j + 1])
            else:
                nc.vector.tensor_scalar(out=dst, in0=src, scalar1=xs[:, j : j + 1], scalar2=None, op0=ALU.mult)

        def batch_half(s, half):
            if s not in batch:
                nm = "batch" if s >= 2 else f"batch{s + 1}"
                batch[s] = work.tile([P, 2, CHUNK, PACK], BF16, name=nm, bufs=1, align_bytes=64)
            return batch[s][:, half]

        def interleave(k, part, parts, eng):
            dst_all = batch_half(k - 1, 0)
            w = CHUNK // parts
            dst = dst_all[:, part * w : (part + 1) * w, :]
            src = planes[k][:, :, part * w : (part + 1) * w].rearrange("p j w -> p w j")
            if eng == "g":
                nc.gpsimd.tensor_scalar(out=dst, in0=src, scalar1=1.0, scalar2=0.0, op0=ALU.mult, op1=ALU.add)
            elif eng == "s":
                nc.scalar.copy(out=dst, in_=src)
            else:
                nc.vector.tensor_copy(out=dst, in_=src)

        def quantize_half(s, h):
            if h == 0:
                codes = work.tile([P, 2, CHUNK], U32, name="codes", align_bytes=64)
                scales = work.tile([P, 2, CHUNK], U8, name="scales", align_bytes=64)
                gcodes[s - 2] = (codes[:, 1], scales[:, 1])
            codes, scales = gcodes[s - 2]
            cols = slice(h * 256, (h + 1) * 256)
            nc.vector.quantize_mx(out=codes[:, cols].bitcast(FP8X4), scales=scales[:, cols], in_=batch[s][:, 1, cols].rearrange("p w j -> p (w j)"))

        def quantize(s):
            lo = 0 if s + 1 < NCHUNKS else 1
            hi = 2 if s - 2 >= 0 else 1
            codes = work.tile([P, 2, CHUNK], U32, name="codes", align_bytes=64)
            scales = work.tile([P, 2, CHUNK], U8, name="scales", align_bytes=64)
            nc.vector.quantize_mx(
                out=codes[:, lo:hi].rearrange("p h w -> p (h w)").bitcast(FP8X4),
                scales=scales[:, lo:hi].rearrange("p h w -> p (h w)"),
                in_=batch.pop(s)[:, lo:hi].rearrange("p h w j -> p (h w j)"),
            )
            if lo == 0:
                xcodes[s + 1] = (codes[:, 0], scales[:, 0])
            if hi == 2:
                gcodes[s - 2] = (codes[:, 1], scales[:, 1])

        warm = keep.tile([P, 1], F32, name="warm")
        nc.vector.memset(warm[:], 1.0)
        nc.scalar.activation(out=warm[:], in_=warm[:], func=ACT.Abs_reciprocal_sqrt)
        ident = keep.tile([P, P], F32, name="ident", align_bytes=64)
        make_identity(nc, ident[:])
        ident_b = keep.tile([P, P], BF16, name="ident_b", align_bytes=64)
        nc.vector.tensor_copy(out=ident_b[:], in_=ident[:])
        sel = keep.tile([P, BLK], F32, name="sel")
        nc.vector.tensor_reduce(out=sel[:], in_=ident[:].rearrange("p (q i) -> p i q", q=Q), axis=AXIS.X, op=ALU.add)
        pieces = keep.tile([P, NTILES // BLK, Q, BLK], BF16, name="pieces", align_bytes=64)
        nc.vector.memset(pieces[:], 0.0)

        mrow32 = keep.tile([P, P], F32, name="mrow32", align_bytes=64)
        nc.vector.tensor_copy(out=mrow32[:], in_=mrow[:])
        m_ps = psum.tile([P, P], F32, name="m_ps", tag="tr")
        nc.tensor.transpose(m_ps[:], mrow32[:], ident[:])
        m = keep.tile([P, NTILES], F32, name="m")
        nc.scalar.copy(out=m[:], in_=m_ps[:, 0:NTILES])
        t1 = keep.tile([P, NTILES], F32, name="t1")
        t2 = keep.tile([P, NTILES], F32, name="t2")
        t3 = keep.tile([P, NTILES], F32, name="t3")
        t4 = keep.tile([P, NTILES], F32, name="t4")
        sg = keep.tile([P, NTILES], F32, name="sg")
        inv_sg = keep.tile([P, NTILES], F32, name="inv_sg")
        v = keep.tile([P, 2, NTILES], F32, name="v")
        rest = [keep.tile([P, 2, NTILES], F32, name=f"rest{i}") for i in range(2)]

        def g_affine(dst, src, a, b):
            nc.gpsimd.tensor_scalar(out=dst, in0=src, scalar1=a, scalar2=b, op0=ALU.mult, op1=ALU.add)

        widen(0, 1, 0, "s")
        widen(0, 1, 1, "v")
        widen(0, 1, 2, "v")
        nc.vector.tensor_scalar(out=t1[:], in0=m[:], scalar1=1.4, scalar2=-1.7, op0=ALU.mult, op1=ALU.add)
        nc.vector.tensor_scalar(out=t3[:], in0=m[:], scalar1=0.7, scalar2=None, op0=ALU.mult)
        widen(0, 1, 3, "v")
        nc.vector.tensor_mul(out=t2[:], in0=t1[:], in1=m[:])
        nc.vector.tensor_mul(out=t4[:], in0=t3[:], in1=m[:])
        interleave(0, 0, 2, "v")
        nc.vector.tensor_scalar(out=sg[:], in0=t2[:], scalar1=1.0, scalar2=None, op0=ALU.add)
        interleave(0, 1, 2, "v")
        nc.vector.reciprocal(out=inv_sg[:], in_=sg[:])

        wq_grouped = keep.tile([P, C, PACK], BF16, name="wq_grouped", align_bytes=64)
        wq_codes = keep.tile([P, C], U32, name="wq_codes", align_bytes=64)
        wq_scales = keep.tile([P, C], U8, name="wq_scales", align_bytes=64)

        def permute_wq(u, eng):
            dst = wq_grouped[:, u * 256 : (u + 1) * 256, :].rearrange("p (m e) j -> p m e j", e=2)
            src = wq_raw[:].rearrange("p j (m u e) -> p u m e j", u=2, e=2)[:, u]
            if eng == "g":
                g_affine(dst, src, 1.0, 0.0)
            else:
                nc.scalar.copy(out=dst, in_=src)

        permute_wq(0, "s")
        permute_wq(1, "s")
        nc.gpsimd.tensor_mul(out=v[:, 1, :], in0=t4[:], in1=inv_sg[:])
        quantize(-1)
        bq = keep.tile([P, C], BF16, name="bq")
        nc.scalar.copy(out=bq[:].rearrange("p (u m e) -> p u m e", u=2, e=2), in_=bq_raw[:].rearrange("p (m u e) -> p u m e", u=2, e=2))


        def piece(i):
            res = v if i == 0 else rest[i - 1]
            for h in range(2):
                src = res[:, h, :].rearrange("p (b i) -> p b i", i=BLK)
                g_affine(pieces[:, :, 3 * h + i, :], src, 1.0, 0.0)
                if i < 2:
                    nc.gpsimd.tensor_sub(out=rest[i][:, h, :].rearrange("p (b i) -> p b i", i=BLK), in0=src, in1=pieces[:, :, 3 * h + i, :])

        nc.vector.quantize_mx(out=wq_codes[:].bitcast(FP8X4), scales=wq_scales[:], in_=wq_grouped[:].rearrange("p w j -> p (w j)"))
        for j in range(PACK):
            widen(1, 1, j, "v")

        q0 = {}
        gate = {}
        qb = {}
        ss = {}
        rn = {}
        gt = {}
        tr = {}
        y_ps = {}

        def mm1(k, i):
            codes, scales = xcodes[k]
            cols = slice(i * TILE, (i + 1) * TILE)
            q0[k, i] = psum.tile([P, C], F32, name="q0")
            nc.tensor.matmul_mx(out=q0[k, i][:], lhsT=codes[:, cols].bitcast(FP8X4), lhsT_scale=scales[:, cols],
                                rhs=wq_codes[:].bitcast(FP8X4), rhs_scale=wq_scales[:], start=True, stop=True)

        mm1(0, 0)
        mm1(0, 1)

        pt = keep.tile([P, 4, P], BF16, name="pt", align_bytes=64)
        ptm = keep.tile([P, BLK, 4, P], BF16, name="ptm", align_bytes=64)

        def turn_pieces():
            ps = psum.tile([P, 4, P], BF16, name="pt_ps", tag="tr")
            for b in range(4):
                nc.tensor.transpose(ps[:, b, :], pieces[:, b].rearrange("p q i -> p (q i)"), ident_b[:])
            nc.scalar.copy(out=pt[:], in_=ps[:])

        def mask_pieces(ii):
            nc.vector.tensor_scalar(out=ptm[:, ii], in0=pt[:], scalar1=sel[:, ii : ii + 1], scalar2=None, op0=ALU.mult)

        interleave(1, 0, 2, "g")
        interleave(1, 1, 2, "g")

        kv_rows = []

        def permute_rows(img):
            r = keep.tile([P, C], BF16, name=f"kv_rows{img}", align_bytes=64)
            nc.scalar.copy(out=r[:].rearrange("p (u m e) -> p u m e", u=2, e=2), in_=kv_raw[img][:].rearrange("p (m u e) -> p u m e", u=2, e=2))
            kv_rows.append(r)

        kcol = keep.tile([P, 4], F32, name="kcol")
        dcol = keep.tile([P, 4], F32, name="dcol")

        def take_columns():
            ps = psum.tile([P, 4, P], BF16, name="kv_ps", tag="tr")
            for r in range(4):
                nc.tensor.transpose(ps[:, r, :], kv_rows[0][:, r * P : (r + 1) * P], ident_b[:])
            nc.vector.tensor_copy(out=kcol[:], in_=ps[:, :, 0])
            nc.vector.tensor_sub(out=dcol[:], in0=ps[:, :, 48], in1=kcol[:])

        gate_t = {}

        def spread_rho(todo):
            ps = psum.tile([P, 4, TILE], F32, name="rho_ps", tag="tr")
            for n, (k, i) in enumerate(todo):
                t = k * NT + i
                nc.tensor.transpose(ps[:, n, :], v[:, 1, t : t + 1].to_broadcast([P, P]), ident[:])
            return ps

        def gate_columns(todo, ps, first=0):
            for n, (k, i) in enumerate(todo, first):
                gate_t[k, i] = keep.tile([P, 4, TILE], F32, name=f"gate_t{k}_{i}", align_bytes=64)
                for r in range(4):
                    nc.scalar.activation(out=gate_t[k, i][:, r, :], in_=ps[:, n, :], func=ACT.Identity, scale=dcol[:, r : r + 1], bias=kcol[:, r : r + 1])

        wo_grouped = keep.tile([P, C, PACK], BF16, name="wo_grouped", align_bytes=64)
        wo_codes = keep.tile([P, C], U32, name="wo_codes", align_bytes=64)
        wo_scales = keep.tile([P, C], U8, name="wo_scales", align_bytes=64)


        def make_gate(k, i):
            t = k * NT + i
            img = k // PER_IMG
            gate[k, i] = psum.tile([P, C], F32, name="gate")
            if (k, i) in TURNED_GATES:
                for r in range(4):
                    nc.tensor.transpose(gate[k, i][:, r * P : (r + 1) * P], gate_t[k, i][:, r, :], ident[:])
            else:
                nc.tensor.matmul(gate[k, i][:], lhsT=ptm[:, t % BLK, t // BLK, :], rhs=kv_rows[img][:], start=True, stop=True)

        def add_bias(k, i):
            qb[k, i] = work.tile([P, C], F32, name="qb", bufs=10)
            nc.vector.tensor_add(out=qb[k, i][:], in0=q0.pop((k, i))[:], in1=bq[:])

        def squares(k, i):
            if k not in ss:
                ss[k] = work.tile([P, NT], F32, name="ss")
            t = k * NT + i
            junk = work.tile([P, C], BF16, name="junk", bufs=8)
            nc.scalar.activation(out=junk[:], in_=qb[k, i][:], func=ACT.Square, scale=inv_sg[:, t : t + 1], accum_out=ss[k][:, i : i + 1])

        def root(k):
            rn[k] = work.tile([P, NT], F32, name="rn")
            nc.scalar.activation(out=rn[k][:], in_=ss[k][:], func=ACT.Abs_reciprocal_sqrt)

        def gating(k, i):
            gt[k, i] = work.tile([P, C], BF16, name="gt", bufs=6, align_bytes=64)
            nc.vector.scalar_tensor_tensor(out=gt[k, i][:], in0=gate.pop((k, i))[:], scalar=rn[k][:, i : i + 1], in1=qb.pop((k, i))[:], op0=ALU.mult, op1=ALU.mult)

        def turn(k, h):
            tr[k, h] = psum.tile([P, 2, 2, TILE], F32, name="tr", tag="tr")
            for a in range(2):
                words = gt.pop((k, 2 * h + a))[:].bitcast(F32)
                for u in range(2):
                    nc.tensor.transpose(tr[k, h][:, a, u, :], words[:, u * 128 : (u + 1) * 128], ident[:])

        def unload(k, h):
            dst = batch_half(k + 2, 1).rearrange("p w j -> p (w j)").bitcast(F32)[:, h * 512 : (h + 1) * 512]
            nc.scalar.copy(out=dst.rearrange("p (a r u) -> p a r u", a=2, u=2), in_=tr.pop((k, h))[:].rearrange("p a u r -> p a r u"))

        def mm2(k, i):
            codes, scales = gcodes[k]
            cols = slice(i * TILE, (i + 1) * TILE)
            y_ps[k, i] = psum.tile([P, C], F32, name="y_ps")
            nc.tensor.matmul_mx(out=y_ps[k, i][:], lhsT=codes[:, cols].bitcast(FP8X4), lhsT_scale=scales[:, cols],
                                rhs=wo_codes[:].bitcast(FP8X4), rhs_scale=wo_scales[:], start=True, stop=True)

        y_sb = {}

        def finish(k, i, eng):
            h = i // 2
            if (k, h) not in y_sb:
                y_sb[k, h] = work.tile([P, 2, C], F32, name=f"y{h}", bufs=3)
            y = y_sb[k, h][:, i % 2, :]
            src = y_ps.pop((k, i))
            if eng == "v":
                nc.vector.tensor_add(out=y, in0=src[:], in1=bo[:])
            else:
                nc.scalar.copy(out=y, in_=src[:])

        def add_out(k, i):
            y = y_sb[k, i // 2][:, i % 2, :]
            nc.gpsimd.tensor_add(out=y, in0=y, in1=bo[:])

        def store(k, h):
            t0 = (k * NT + 2 * h) * TILE
            nc.sync.dma_start(out=out_rows[t0 : t0 + 2 * TILE, :].rearrange("(a p) c -> p a c", p=P), in_=y_sb.pop((k, h))[:])

        def store_one(k, i):
            t0 = (k * NT + i) * TILE
            nc.sync.dma_start(out=out_rows[t0 : t0 + TILE, :], in_=y_sb[k, i // 2][:, i % 2, :])

        def step(s):
            new = s < NCHUNKS
            mid = 0 <= s - 1 < NCHUNKS
            old = 0 <= s - 2 < NCHUNKS
            fill = s + 2 < NCHUNKS
            pair = s + 4 - s % 2
            todo = [g for g in TURNED_GATES if g[0] == s]
            if s in V_WIDENS:
                widen(pair, 2, 3, "v")
            if s >= 2:
                quantize(s)
            if s == 2:
                nc.vector.quantize_mx(out=wo_codes[:].bitcast(FP8X4), scales=wo_scales[:], in_=wo_grouped[:].rearrange("p w j -> p (w j)"))
            if s >= 2 and pair < NCHUNKS:
                widen(pair, 2, 2 * (s % 2), "s")
                if s not in V_WIDENS:
                    widen(pair, 2, 2 * (s % 2) + 1, "s")
            if fill and s >= 2:
                interleave(s + 2, 0, 2, "g")
                interleave(s + 2, 1, 2, "g")
            if old:
                mm2(s - 2, 0)
                mm2(s - 2, 1)
            if s <= 1:
                add_bias(s, 0)
                add_bias(s, 1)
            if s == 0:
                take_columns()
                rho0 = spread_rho(todo)
                gate_columns(todo[:2], rho0)
            if mid:
                gating(s - 1, 1)
                gating(s - 1, 0)
                make_gate(s - 1, 2)
                make_gate(s - 1, 3)
                turn(s - 1, 0)
            by_scalar = (1,) if s in LIGHT else (1, 0)
            if old:
                for i in by_scalar:
                    finish(s - 2, i, "s")
                    add_out(s - 2, i)
            if mid and s >= 2:
                unload(s - 1, 0)
            if new and s >= 2:
                add_bias(s, 0)
                add_bias(s, 1)
            if new:
                mm1(s, 2)
                mm1(s, 3)
                squares(s, 1)
                squares(s, 0)
            if s == 1:
                unload(0, 0)
            if s == 2:
                turn_pieces()
            if old and 0 not in by_scalar:
                finish(s - 2, 0, "v")
            if old:
                mm2(s - 2, 2)
                mm2(s - 2, 3)
            if mid:
                gating(s - 1, 3)
                gating(s - 1, 2)
                turn(s - 1, 1)
                unload(s - 1, 1)
            if new:
                add_bias(s, 3)
                add_bias(s, 2)
                squares(s, 3)
                squares(s, 2)
                root(s)
            if s <= 1:
                for j in range(2):
                    widen(2 * s + 2, 2, 2 + j, "v")
                quantize(s)
            if s == 0:
                for i in range(4):
                    interleave(2 + i // 2, i % 2, 2, "g")
                g_affine(v[:, 0, :], v[:, 1, :], -1.0, 1.0)
                for i in range(3):
                    piece(i)
            if s == 2:
                for ii in range(8, 12):
                    mask_pieces(ii)
            if s + 1 < NCHUNKS:
                mm1(s + 1, 0)
                mm1(s + 1, 1)
            if todo:
                if s == 0:
                    gate_columns(todo[2:], rho0, 2)
                else:
                    gate_columns(todo, spread_rho(todo))
            if new:
                make_gate(s, 0)
                make_gate(s, 1)
            if s == 0:
                widen(4, 2, 0, "s")
                widen(4, 2, 1, "s")
            if old:
                for i in (3, 2):
                    finish(s - 2, i, "v")
                store(s - 2, 0)
                store(s - 2, 1)
            if s in (2, 3, 4):
                for ii in [(12, 13, 14, 15), (0, 1, 2, 3), (4, 5, 6, 7)][s - 2]:
                    mask_pieces(ii)
            if s == 1:
                nc.vector.tensor_copy(out=wo_grouped[:], in_=wo_raw[:].rearrange("p j w -> p w j"))
            if s == 5:
                permute_rows(1)

        def last_steps():
            k = NCHUNKS - 1
            s = NCHUNKS
            quantize(s)
            mm2(k - 1, 0)
            mm2(k - 1, 1)
            gating(k, 1)
            gating(k, 0)
            make_gate(k, 2)
            make_gate(k, 3)
            turn(k, 0)
            finish(k - 1, 1, "s")
            add_out(k - 1, 1)
            unload(k, 0)
            finish(k - 1, 0, "v")
            store(k - 1, 0)
            mm2(k - 1, 2)
            mm2(k - 1, 3)
            gating(k, 3)
            gating(k, 2)
            turn(k, 1)
            unload(k, 1)
            quantize_half(s + 1, 0)
            mm2(k, 0)
            mm2(k, 1)
            finish(k - 1, 3, "v")
            finish(k - 1, 2, "v")
            store(k - 1, 1)
            quantize_half(s + 1, 1)
            finish(k, 0, "s")
            add_out(k, 0)
            finish(k, 1, "v")
            mm2(k, 2)
            mm2(k, 3)
            store_one(k, 1)
            finish(k, 2, "v")
            store_one(k, 0)
            finish(k, 3, "v")
            store_one(k, 2)
            store_one(k, 3)

        permute_rows(0)
        widen(2, 2, 0, "s")
        widen(2, 2, 1, "s")
        for s in range(NCHUNKS):
            step(s)
        last_steps()
